import numpy as np
import ml_dtypes


def mxq(x, axis, fmt="e4m3"):
    dtype, down = {"e4m3": (ml_dtypes.float8_e4m3fn, 7), "e5m2": (ml_dtypes.float8_e5m2, 14)}[fmt]
    v = np.moveaxis(np.asarray(x, np.float32).astype(ml_dtypes.bfloat16).astype(np.float64), axis, -1)
    blocks = v.reshape(v.shape[:-1] + (-1, 32))
    amax = np.abs(blocks).max(-1, keepdims=True)
    byte = np.maximum(np.where(amax > 0, np.frexp(amax)[1] - 1 + 127, 0) - down, 1)
    scale = np.exp2(byte - 127.0)
    codes = (blocks / scale).astype(np.float32).astype(dtype).astype(np.float64)
    return np.moveaxis((codes * scale).reshape(v.shape), -1, axis)


WIDE = False


def mx_kscale(k):
    if not WIDE:
        return np.ones(k)
    levels = np.array([10, -10, 5, -5, 0])
    if k % 512:
        return np.exp2(np.random.permutation(np.resize(levels, k // 32))).repeat(32)
    a = np.empty((k // 512, 16))
    for p in range(k // 512):
        a[p, :8] = np.random.permutation(np.resize(levels, 8))
        for g in range(8):
            far = levels[np.abs(levels - a[p, g]) >= 10]
            a[p, g + 8] = far[np.random.randint(len(far))]
    return np.exp2(a.ravel()).repeat(32)


BF16 = ml_dtypes.bfloat16


def bf(x):
    return np.asarray(x, np.float32).astype(BF16)


def f64(x):
    return np.asarray(x).astype(np.float64)


B, T, KA, KT, DIM, NH, HD, E = 16, 512, 256, 256, 512, 8, 128, 8
EPS = 1e-5


def setup_inputs():
    r = np.random.standard_normal
    s = mx_kscale(DIM)
    t = mx_kscale(DIM)
    return {"h_attn": bf(r((B, T, DIM)) * 0.4 * s),
            "x": bf(r((B, T, DIM))),
            "W_o": bf(r((DIM, DIM)) * 2.0 / np.sqrt(DIM) / s[None, :]),
            "b_o": bf(r(DIM) * 0.3 + 0.2),
            "W_ffn": bf(r((DIM, DIM)) / np.sqrt(DIM) / t[None, :]),
            "b_ffn": bf(r(DIM) * 0.3),
            "gamma": bf((1.0 + 0.1 * r(DIM)) * t),
            "beta": bf(0.2 * r(DIM) * t)}


def reference(h_attn, x, W_o, b_o, W_ffn, b_ffn, gamma, beta):
    y = (mxq(f64(h_attn), 2, "e4m3") @ mxq(f64(W_o), 1, "e4m3").T) + f64(b_o) + f64(x)
    mu = y.mean(-1, keepdims=True)
    var = ((y - mu) ** 2).mean(-1, keepdims=True)
    xn = (y - mu) / np.sqrt(var + EPS) * f64(gamma) + f64(beta)
    return np.maximum((mxq(xn, 2, "e4m3") @ mxq(f64(W_ffn), 1, "e4m3").T) + f64(b_ffn), 0.0)

@@ -1,0 +1,330 @@
+from contextlib import ExitStack
+
+import concourse.mybir as mybir
+from concourse.masks import make_identity
+
+F32 = mybir.dt.float32
+BF16 = mybir.dt.bfloat16
+U32 = mybir.dt.uint32
+U8 = mybir.dt.uint8
+FP8X4 = mybir.dt.float8_e4m3fn_x4
+ALU = mybir.AluOpType
+ACT = mybir.ActivationFunctionType
+
+P = 128
+DIM = 512
+TOKENS = 16 * 512
+CH = 8
+NCH = TOKENS // (P * CH)
+NPAIR = TOKENS // (2 * P)
+EPS = 1e-5
+FLOPS = 2 * 2 * TOKENS * DIM * DIM
+
+MANUAL = False
+NQUAD = NPAIR // 2
+
+
+def tile_l1regressionmoeactionhead_pc_t_kernel(tc, h_attn, x, W_o, b_o, W_ffn, b_ffn, gamma, beta, out):
+    nc = tc.nc
+    hv = h_attn.flatten_outer_dims().rearrange("(c p j) k -> c p j k", p=P, j=CH)
+    xv = x.flatten_outer_dims().rearrange("(c p j) k -> c p j k", p=P, j=CH)
+    ov = out.flatten_outer_dims().rearrange("(c p j) k -> c p j k", p=P, j=CH)
+
+    with ExitStack() as ctx:
+        const = ctx.enter_context(tc.tile_pool(name="const", bufs=1))
+        loads = ctx.enter_context(tc.tile_pool(name="loads", bufs=3))
+        work = ctx.enter_context(tc.tile_pool(name="work", bufs=2))
+        stats = ctx.enter_context(tc.tile_pool(name="stats", bufs=4))
+        psum = ctx.enter_context(tc.psum_pool(name="psum", bufs=2))
+        if MANUAL:
+            ctx.enter_context(tc.manual_schedule())
+
+        h_tiles = {}
+        x_tiles = {}
+
+        def load_h(c, pieces):
+            h_sb = loads.tile([P, CH, DIM], BF16, tag="h", name="h_sb")
+            h_tiles[c] = h_sb
+            step = CH // pieces
+            for i in range(pieces):
+                nc.sync.dma_start(out=h_sb[:, i * step:(i + 1) * step, :], in_=hv[c][:, i * step:(i + 1) * step, :])
+
+        def load_x(c, pieces):
+            x_sb = loads.tile([P, CH, DIM], BF16, tag="x", name="x_sb")
+            x_tiles[c] = x_sb
+            step = CH // pieces
+            for i in range(pieces):
+                nc.sync.dma_start(out=x_sb[:, i * step:(i + 1) * step, :], in_=xv[c][:, i * step:(i + 1) * step, :])
+
+        bo_b = const.tile([P, DIM], BF16)
+        nc.scalar.dma_start(out=bo_b[:], in_=b_o.partition_broadcast(P))
+        def load_part(tiles, view, tag, c, j0, j1):
+            if j0 == 0:
+                fresh = loads.tile([P, CH, DIM], BF16, tag=tag, name="ld_" + tag)
+                tiles[c] = fresh
+            nc.sync.dma_start(out=tiles[c][:, j0:j1, :], in_=view[c][:, j0:j1, :])
+
+        load_part(x_tiles, xv, "x", 0, 0, 4)
+        wo_sb = const.tile([P, 4, DIM], BF16)
+        nc.sync.dma_start(out=wo_sb[:], in_=W_o.rearrange("(r p) k -> p r k", p=P))
+        load_part(h_tiles, hv, "h", 0, 0, 2)
+        load_part(h_tiles, hv, "h", 0, 2, 4)
+        load_part(x_tiles, xv, "x", 0, 4, 8)
+        load_part(h_tiles, hv, "h", 0, 4, 8)
+        load_part(x_tiles, xv, "x", 1, 0, 4)
+        g_raw = const.tile([P, 4], BF16)
+        nc.scalar.dma_start(out=g_raw[:], in_=gamma.rearrange("(p t) -> p t", t=4))
+        b_raw = const.tile([P, 4], BF16)
+        nc.scalar.dma_start(out=b_raw[:], in_=beta.rearrange("(p t) -> p t", t=4))
+        wf_sb = const.tile([P, 4, DIM], BF16)
+        nc.sync.dma_start(out=wf_sb[:], in_=W_ffn.rearrange("(r p) k -> p r k", p=P))
+        bf_b = const.tile([P, DIM], BF16)
+        nc.scalar.dma_start(out=bf_b[:], in_=b_ffn.partition_broadcast(P))
+        load_part(h_tiles, hv, "h", 1, 0, 8)
+        load_part(x_tiles, xv, "x", 1, 4, 8)
+        load_h(2, 1)
+        load_x(2, 1)
+
+        ident_f = const.tile([P, P], F32)
+        make_identity(nc, ident_f[:])
+        ident_b = const.tile([P, P], BF16)
+        make_identity(nc, ident_b[:])
+        eps_t = const.tile([P, 1], F32)
+        nc.vector.memset(eps_t[:], EPS)
+        warm = const.tile([P, 1], F32)
+        nc.scalar.activation(out=warm[:], in_=eps_t[:], func=ACT.Abs_reciprocal_sqrt)
+
+        S = {}
+
+        def st_xp(q):
+            xp = work.tile([P, 4, DIM], F32, tag="xp", bufs=3, name="xp")
+            S[("xp", q)] = xp
+            j0 = (q % 2) * 4
+            nc.vector.tensor_tensor(out=xp[:], in0=x_tiles[q // 2][:, j0:j0 + 4, :], in1=bo_b[:].unsqueeze(1).to_broadcast([P, 4, DIM]), op=ALU.add)
+
+        st_xp(0)
+
+        wog = const.tile([P, DIM * 4], BF16, align_bytes=64)
+        woc = const.tile([P, DIM], U32, align_bytes=64)
+        wos = const.tile([P, DIM], U8, align_bytes=64)
+        wog_w = wog[:].bitcast(F32).rearrange("p (r c u) -> p r c u", r=4, u=2)
+        for half in range(2):
+            wt = psum.tile([P, 2, 2, P], F32, tag="ht", name="wt")
+            for rr in range(2):
+                for u in range(2):
+                    nc.tensor.transpose(wt[:, rr, u, :], wo_sb[:, 2 * half + rr, :].bitcast(F32)[:, u::2], ident_f[:])
+            nc.scalar.copy(out=wog_w[:, 2 * half:2 * half + 2, :, :], in_=wt[:].rearrange("p j u r -> p j r u"))
+        nc.vector.quantize_mx(out=woc[:].bitcast(FP8X4), scales=wos[:], in_=wog[:])
+        st_xp(1)
+
+        gb = const.tile([P, 8], F32)
+        wfg = const.tile([P, DIM, 4], BF16, align_bytes=64)
+        wfc = const.tile([P, DIM], U32, align_bytes=64)
+        wfs = const.tile([P, DIM], U8, align_bytes=64)
+
+        def prep_wf_transposes():
+            for r in range(4):
+                wt2 = psum.tile([P, 4, P], BF16, tag="p2", name="wt2")
+                for t in range(4):
+                    nc.tensor.transpose(wt2[:, t, :], wf_sb[:, r, t::4], ident_b[:])
+                nc.scalar.copy(out=wfg[:, r * P:(r + 1) * P, :], in_=wt2[:].rearrange("p t c -> p c t"))
+
+        def prep_wf_quantise():
+            nc.vector.tensor_copy(out=gb[:, 0:4], in_=g_raw[:])
+            nc.vector.tensor_copy(out=gb[:, 4:8], in_=b_raw[:])
+            nc.vector.quantize_mx(out=wfc[:].bitcast(FP8X4), scales=wfs[:], in_=wfg[:].rearrange("p c t -> p (c t)"))
+
+        def st_th(pr):
+            ht = psum.tile([P, 2, 2, P], F32, tag="ht", name="ht")
+            S[("ht", pr)] = ht
+            for jj in range(2):
+                hsrc = h_tiles[pr // 4][:, (pr % 4) * 2 + jj, :]
+                for u in range(2):
+                    nc.tensor.transpose(ht[:, jj, u, :], hsrc.bitcast(F32)[:, u::2], ident_f[:])
+
+        def st_a(pr):
+            q = pr // 2
+            if pr % 2 == 0:
+                hg_new = work.tile([P, 4 * DIM], BF16, tag="hg", bufs=4, align_bytes=64, name="hg")
+                S[("hg", q)] = hg_new
+            hg = S[("hg", q)]
+            j0 = (pr % 2) * 2
+            nc.scalar.copy(out=hg[:].bitcast(F32).rearrange("p (j r u) -> p j r u", j=4, u=2)[:, j0:j0 + 2, :, :],
+                           in_=S[("ht", pr)][:].rearrange("p j u r -> p j r u"))
+
+        def st_qh(q):
+            hc = work.tile([P, 4 * P], U32, tag="hc", bufs=3, align_bytes=64, name="hc")
+            hs = work.tile([P, 4 * P], U8, tag="hs", bufs=3, align_bytes=64, name="hs")
+            S[("hc", q)] = (hc, hs)
+            nc.vector.quantize_mx(out=hc[:].bitcast(FP8X4), scales=hs[:], in_=S[("hg", q)][:])
+
+        def st_mx1(pr):
+            hc, hs = S[("hc", pr // 2)]
+            for jj in range(2):
+                c0 = ((pr % 2) * 2 + jj) * P
+                p1 = psum.tile([P, DIM], F32, tag="p1", name="p1")
+                S[("p1", pr, jj)] = p1
+                nc.tensor.matmul_mx(out=p1[:], lhsT=hc[:, c0:c0 + P].bitcast(FP8X4), lhsT_scale=hs[:, c0:c0 + P],
+                                    rhs=woc[:].bitcast(FP8X4), rhs_scale=wos[:], start=True, stop=True)
+
+        def st_c(pr):
+            q = pr // 2
+            if pr % 2 == 0:
+                sums_new = stats.tile([P, 4], F32, tag="sums", name="sums")
+                S[("sums", q)] = sums_new
+            sums = S[("sums", q)]
+            for jj in range(2):
+                j = (pr % 2) * 2 + jj
+                y = work.tile([P, DIM], F32, tag="y", bufs=20, name="y")
+                S[("y", pr, jj)] = y
+                nc.vector.scalar_tensor_tensor(out=y[:], in0=S[("p1", pr, jj)][:], scalar=0.0, in1=S[("xp", q)][:, j, :],
+                                               op0=ALU.add, op1=ALU.add, accum_out=sums[:, j:j + 1])
+
+        def st_negmu(q):
+            negmu = stats.tile([P, 4], F32, tag="negmu", name="negmu")
+            S[("negmu", q)] = negmu
+            nc.gpsimd.tensor_scalar(out=negmu[:], in0=S[("sums", q)][:], scalar1=-1.0 / DIM, scalar2=0.0, op0=ALU.mult, op1=ALU.add)
+
+        def st_d(pr):
+            q = pr // 2
+            if pr % 2 == 0:
+                ssq_new = stats.tile([P, 4], F32, tag="ssq", name="ssq")
+                S[("ssq", q)] = ssq_new
+            ssq = S[("ssq", q)]
+            negmu = S[("negmu", q)]
+            for jj in range(2):
+                j = (pr % 2) * 2 + jj
+                junk = work.tile([P, DIM], BF16, tag="junk", name="junk")
+                nc.scalar.activation(out=junk[:], in_=S[("y", pr, jj)][:], func=ACT.Square, bias=negmu[:, j:j + 1], scale=1.0,
+                                     accum_out=ssq[:, j:j + 1])
+
+        def st_ars(q):
+            rstd = stats.tile([P, 4], F32, tag="rstd", name="rstd")
+            S[("rstd", q)] = rstd
+            nc.scalar.activation(out=rstd[:], in_=S[("ssq", q)][:], func=ACT.Abs_reciprocal_sqrt, bias=eps_t[:, 0:1], scale=1.0 / DIM)
+
+        def st_nmr(q):
+            nmr = stats.tile([P, 4], F32, tag="nmr", name="nmr")
+            S[("nmr", q)] = nmr
+            nc.gpsimd.tensor_tensor(out=nmr[:], in0=S[("negmu", q)][:], in1=S[("rstd", q)][:], op=ALU.mult)
+
+        def st_e(pr):
+            q = pr // 2
+            for jj in range(2):
+                j = (pr % 2) * 2 + jj
+                y = S[("y", pr, jj)]
+                nc.scalar.activation(out=y[:], in_=y[:], func=ACT.Identity, bias=S[("nmr", q)][:, j:j + 1], scale=S[("rstd", q)][:, j:j + 1])
+
+        def st_tz(s):
+            q = s // 2
+            for tt in range(2):
+                t = 2 * (s % 2) + tt
+                zt = psum.tile([P, 4, P], F32, tag="zt", name="zt")
+                S[("zt", q, t)] = zt
+                for j in range(4):
+                    nc.tensor.transpose(zt[:, j, :], S[("y", 2 * q + j // 2, j % 2)][:, t::4], ident_f[:])
+
+        def st_f(s):
+            q = s // 2
+            if s % 2 == 0:
+                planes_new = work.tile([P, 4, 4 * P], BF16, tag="planes", bufs=3, name="planes")
+                S[("planes", q)] = planes_new
+            planes = S[("planes", q)]
+            for tt in range(2):
+                t = 2 * (s % 2) + tt
+                nc.scalar.activation(out=planes[:, t, :], in_=S[("zt", q, t)][:].rearrange("p j r -> p (j r)"),
+                                     func=ACT.Identity, bias=gb[:, 4 + t:5 + t], scale=gb[:, t:t + 1])
+
+        def st_f2(q):
+            xg = work.tile([P, 4 * P, 4], BF16, tag="xg", bufs=2, align_bytes=64, name="xg")
+            S[("xg", q)] = xg
+            nc.vector.tensor_copy(out=xg[:].rearrange("p (c i) t -> p c t i", i=4),
+                                  in_=S[("planes", q)][:].rearrange("p t (c i) -> p c t i", i=4))
+
+        def st_qx(q):
+            xc = work.tile([P, 4 * P], U32, tag="xc", bufs=3, align_bytes=64, name="xc")
+            xs = work.tile([P, 4 * P], U8, tag="xs", bufs=3, align_bytes=64, name="xs")
+            S[("xc", q)] = (xc, xs)
+            nc.vector.quantize_mx(out=xc[:].bitcast(FP8X4), scales=xs[:], in_=S[("xg", q)][:].rearrange("p c t -> p (c t)"))
+
+        def st_mx2(pr):
+            xc, xs = S[("xc", pr // 2)]
+            for jj in range(2):
+                c0 = ((pr % 2) * 2 + jj) * P
+                p2 = psum.tile([P, DIM], F32, tag="p2", name="p2")
+                S[("p2", pr, jj)] = p2
+                nc.tensor.matmul_mx(out=p2[:], lhsT=xc[:, c0:c0 + P].bitcast(FP8X4), lhsT_scale=xs[:, c0:c0 + P],
+                                    rhs=wfc[:].bitcast(FP8X4), rhs_scale=wfs[:], start=True, stop=True)
+
+        def st_h1(pr):
+            q = pr // 2
+            if pr % 2 == 0:
+                o_new = work.tile([P, 4, DIM], F32, tag="o", bufs=3, name="o")
+                S[("o", q)] = o_new
+            o = S[("o", q)]
+            for jj in range(2):
+                nc.vector.tensor_tensor(out=o[:, (pr % 2) * 2 + jj, :], in0=S[("p2", pr, jj)][:], in1=bf_b[:], op=ALU.add)
+
+        def st_relu(q):
+            o = S[("o", q)]
+            j0 = (q % 2) * 4
+            if q == NQUAD - 1:
+                return
+            if q % 2 == 1:
+                nc.vector.tensor_scalar(out=o[:], in0=o[:], scalar1=0.0, scalar2=None, op0=ALU.max)
+            else:
+                nc.scalar.activation(out=o[:], in_=o[:], func=ACT.Relu)
+            nc.sync.dma_start(out=ov[q // 2][:, j0:j0 + 4, :], in_=o[:])
+
+        def st_relu_last(pr):
+            if pr // 2 != NQUAD - 1:
+                return
+            o = S[("o", pr // 2)]
+            j1 = (pr % 2) * 2
+            if pr % 2 == 0:
+                nc.scalar.activation(out=o[:, j1:j1 + 2, :], in_=o[:, j1:j1 + 2, :], func=ACT.Relu)
+                nc.sync.dma_start(out=ov[pr // 4][:, 4 + j1:4 + j1 + 2, :], in_=o[:, j1:j1 + 2, :])
+            else:
+                nc.scalar.activation(out=o[:, 2, :], in_=o[:, 2, :], func=ACT.Relu)
+                nc.sync.dma_start(out=ov[pr // 4][:, 6, :], in_=o[:, 2, :])
+                nc.vector.tensor_scalar(out=o[:, 3, :], in0=o[:, 3, :], scalar1=0.0, scalar2=None, op0=ALU.max)
+                nc.sync.dma_start(out=ov[pr // 4][:, 7, :], in_=o[:, 3, :])
+
+        def on(fn, pr):
+            if 0 <= pr < NPAIR:
+                fn(pr)
+
+        def onq(fn, m):
+            if m % 2 == 0 and 0 <= m // 2 < NQUAD:
+                fn(m // 2)
+
+        for n in range(NPAIR + 26):
+            if n % 4 == 3 and n >= 7 and n // 4 + 2 < NCH:
+                load_h(n // 4 + 2, 1)
+                load_x(n // 4 + 2, 1)
+            if n == 2:
+                prep_wf_transposes()
+            if n == 3:
+                st_xp(2)
+            if n == 5:
+                prep_wf_quantise()
+            if n >= 10:
+                onq(st_xp, n - 4)
+            onq(st_qx, n - 20)
+            on(st_c, n - 7)
+            on(st_mx1, n - 6)
+            onq(st_qh, n - 5)
+            on(st_h1, n - 22)
+            on(st_mx2, n - 21)
+            onq(st_negmu, n - 8)
+            on(st_e, n - 13)
+            on(st_a, n - 1)
+            on(st_th, n)
+            on(st_d, n - 10)
+            on(st_f, n - 15)
+            on(st_tz, n - 14)
+            onq(st_ars, n - 11)
+            onq(st_nmr, n - 11)
+            onq(st_f2, n - 19)
+            on(st_relu_last, n - 23)
+            onq(st_relu, n - 25)

@@ -10,18 +10,17 @@ U8 = mybir.dt.uint8
 FP8X4 = mybir.dt.float8_e4m3fn_x4
 ALU = mybir.AluOpType
 ACT = mybir.ActivationFunctionType
+ENG = mybir.EngineType
 
 P = 128
 DIM = 512
 TOKENS = 16 * 512
 CH = 8
 NCH = TOKENS // (P * CH)
-NPAIR = TOKENS // (2 * P)
+QT = 4
+NQ = TOKENS // (P * QT)
 EPS = 1e-5
 FLOPS = 2 * 2 * TOKENS * DIM * DIM
-
-MANUAL = False
-NQUAD = NPAIR // 2
 
 
 def tile_l1regressionmoeactionhead_pc_t_kernel(tc, h_attn, x, W_o, b_o, W_ffn, b_ffn, gamma, beta, out):
@@ -36,295 +35,284 @@ def tile_l1regressionmoeactionhead_pc_t_kernel(tc, h_attn, x, W_o, b_o, W_ffn, b
         work = ctx.enter_context(tc.tile_pool(name="work", bufs=2))
         stats = ctx.enter_context(tc.tile_pool(name="stats", bufs=4))
         psum = ctx.enter_context(tc.psum_pool(name="psum", bufs=2))
-        if MANUAL:
-            ctx.enter_context(tc.manual_schedule())
+        ctx.enter_context(tc.manual_schedule(engines={ENG.PE, ENG.Activation, ENG.DVE, ENG.Pool}))
 
         h_tiles = {}
         x_tiles = {}
 
-        def load_h(c, pieces):
-            h_sb = loads.tile([P, CH, DIM], BF16, tag="h", name="h_sb")
-            h_tiles[c] = h_sb
-            step = CH // pieces
-            for i in range(pieces):
-                nc.sync.dma_start(out=h_sb[:, i * step:(i + 1) * step, :], in_=hv[c][:, i * step:(i + 1) * step, :])
-
-        def load_x(c, pieces):
-            x_sb = loads.tile([P, CH, DIM], BF16, tag="x", name="x_sb")
-            x_tiles[c] = x_sb
-            step = CH // pieces
-            for i in range(pieces):
-                nc.sync.dma_start(out=x_sb[:, i * step:(i + 1) * step, :], in_=xv[c][:, i * step:(i + 1) * step, :])
-
-        bo_b = const.tile([P, DIM], BF16)
-        nc.scalar.dma_start(out=bo_b[:], in_=b_o.partition_broadcast(P))
         def load_part(tiles, view, tag, c, j0, j1):
             if j0 == 0:
                 fresh = loads.tile([P, CH, DIM], BF16, tag=tag, name="ld_" + tag)
                 tiles[c] = fresh
             nc.sync.dma_start(out=tiles[c][:, j0:j1, :], in_=view[c][:, j0:j1, :])
 
-        load_part(x_tiles, xv, "x", 0, 0, 4)
         wo_sb = const.tile([P, 4, DIM], BF16)
-        nc.sync.dma_start(out=wo_sb[:], in_=W_o.rearrange("(r p) k -> p r k", p=P))
-        load_part(h_tiles, hv, "h", 0, 0, 2)
-        load_part(h_tiles, hv, "h", 0, 2, 4)
-        load_part(x_tiles, xv, "x", 0, 4, 8)
+        nc.sync.dma_start(out=wo_sb[:], in_=W_o.rearrange("(p t) k -> p t k", t=4))
+        load_part(h_tiles, hv, "h", 0, 0, 4)
+        load_part(x_tiles, xv, "x", 0, 0, 4)
         load_part(h_tiles, hv, "h", 0, 4, 8)
-        load_part(x_tiles, xv, "x", 1, 0, 4)
+        load_part(x_tiles, xv, "x", 0, 4, 8)
+        wf_sb = const.tile([P, 4, DIM], BF16)
+        nc.sync.dma_start(out=wf_sb[:], in_=W_ffn.rearrange("(r p) k -> p r k", p=P))
+        for c in range(1, 3):
+            load_part(h_tiles, hv, "h", c, 0, CH)
+            load_part(x_tiles, xv, "x", c, 0, CH)
+
+        bo_row = const.tile([P, DIM], BF16)
+        nc.vector.memset(bo_row[:], 0.0)
+        nc.scalar.dma_start(out=bo_row[0:1, :], in_=b_o.unsqueeze(0))
+        bf_row = const.tile([P, DIM], BF16)
+        nc.vector.memset(bf_row[:], 0.0)
+        nc.scalar.dma_start(out=bf_row[0:1, :], in_=b_ffn.unsqueeze(0))
         g_raw = const.tile([P, 4], BF16)
         nc.scalar.dma_start(out=g_raw[:], in_=gamma.rearrange("(p t) -> p t", t=4))
         b_raw = const.tile([P, 4], BF16)
         nc.scalar.dma_start(out=b_raw[:], in_=beta.rearrange("(p t) -> p t", t=4))
-        wf_sb = const.tile([P, 4, DIM], BF16)
-        nc.sync.dma_start(out=wf_sb[:], in_=W_ffn.rearrange("(r p) k -> p r k", p=P))
-        bf_b = const.tile([P, DIM], BF16)
-        nc.scalar.dma_start(out=bf_b[:], in_=b_ffn.partition_broadcast(P))
-        load_part(h_tiles, hv, "h", 1, 0, 8)
-        load_part(x_tiles, xv, "x", 1, 4, 8)
-        load_h(2, 1)
-        load_x(2, 1)
 
         ident_f = const.tile([P, P], F32)
         make_identity(nc, ident_f[:])
-        ident_b = const.tile([P, P], BF16)
-        make_identity(nc, ident_b[:])
+        ones = const.tile([P, P], BF16)
+        nc.vector.memset(ones[:], 1.0)
         eps_t = const.tile([P, 1], F32)
         nc.vector.memset(eps_t[:], EPS)
         warm = const.tile([P, 1], F32)
         nc.scalar.activation(out=warm[:], in_=eps_t[:], func=ACT.Abs_reciprocal_sqrt)
 
-        S = {}
+        bo_p = const.tile([P, DIM], BF16)
+        bf_b = const.tile([P, DIM], BF16)
+        gb = const.tile([P, 8], F32)
 
-        def st_xp(q):
-            xp = work.tile([P, 4, DIM], F32, tag="xp", bufs=3, name="xp")
-            S[("xp", q)] = xp
-            j0 = (q % 2) * 4
-            nc.vector.tensor_tensor(out=xp[:], in0=x_tiles[q // 2][:, j0:j0 + 4, :], in1=bo_b[:].unsqueeze(1).to_broadcast([P, 4, DIM]), op=ALU.add)
+        def weight_transposes(w_sb, half, tag):
+            wt = psum.tile([P, 4, P], F32, tag=tag, name="wt")
+            for rr in range(2):
+                for u in range(2):
+                    nc.tensor.transpose(wt[:, 2 * rr + u, :], w_sb[:, 2 * half + rr, :].bitcast(F32)[:, u::2], ident_f[:])
+            return wt
 
-        st_xp(0)
+        def weight_words(grouped, half):
+            return grouped[:].bitcast(F32).rearrange("p (r c u) -> p r c u", r=4, u=2)[:, 2 * half:2 * half + 2, :, :]
+
+        def interleaved(wt):
+            return wt[:].rearrange("p (r u) c -> p r c u", u=2)
 
         wog = const.tile([P, DIM * 4], BF16, align_bytes=64)
         woc = const.tile([P, DIM], U32, align_bytes=64)
         wos = const.tile([P, DIM], U8, align_bytes=64)
-        wog_w = wog[:].bitcast(F32).rearrange("p (r c u) -> p r c u", r=4, u=2)
-        for half in range(2):
-            wt = psum.tile([P, 2, 2, P], F32, tag="ht", name="wt")
-            for rr in range(2):
-                for u in range(2):
-                    nc.tensor.transpose(wt[:, rr, u, :], wo_sb[:, 2 * half + rr, :].bitcast(F32)[:, u::2], ident_f[:])
-            nc.scalar.copy(out=wog_w[:, 2 * half:2 * half + 2, :, :], in_=wt[:].rearrange("p j u r -> p j r u"))
-        nc.vector.quantize_mx(out=woc[:].bitcast(FP8X4), scales=wos[:], in_=wog[:])
-        st_xp(1)
-
-        gb = const.tile([P, 8], F32)
-        wfg = const.tile([P, DIM, 4], BF16, align_bytes=64)
+        wfg = const.tile([P, DIM * 4], BF16, align_bytes=64)
         wfc = const.tile([P, DIM], U32, align_bytes=64)
         wfs = const.tile([P, DIM], U8, align_bytes=64)
 
-        def prep_wf_transposes():
-            for r in range(4):
-                wt2 = psum.tile([P, 4, P], BF16, tag="p2", name="wt2")
-                for t in range(4):
-                    nc.tensor.transpose(wt2[:, t, :], wf_sb[:, r, t::4], ident_b[:])
-                nc.scalar.copy(out=wfg[:, r * P:(r + 1) * P, :], in_=wt2[:].rearrange("p t c -> p c t"))
+        wt_a = weight_transposes(wo_sb, 0, "zt")
+        wt_b = weight_transposes(wo_sb, 1, "zt")
+        bo_ps = psum.tile([P, DIM], F32, tag="p2", name="bo_ps")
+        nc.tensor.matmul(bo_ps[:], lhsT=ones[:], rhs=bo_row[:], start=True, stop=True)
+        nc.vector.tensor_copy(out=weight_words(wog, 0), in_=interleaved(wt_a))
+        nc.scalar.copy(out=weight_words(wog, 1), in_=interleaved(wt_b))
+        nc.vector.tensor_copy(out=bo_p[:].rearrange("p (t m) -> p t m", t=4), in_=bo_ps[:].rearrange("p (m t) -> p t m", t=4))
+        nc.vector.quantize_mx(out=woc[:].bitcast(FP8X4), scales=wos[:], in_=wog[:])
 
-        def prep_wf_quantise():
+        wf_ps = []
+
+        def prep_wf_transposes():
+            for half in range(2):
+                wf_ps.append(weight_transposes(wf_sb, half, "zt"))
+
+        def prep_wf_copies():
+            bf_ps = psum.tile([P, DIM], F32, tag="p2", name="bf_ps")
+            nc.tensor.matmul(bf_ps[:], lhsT=ones[:], rhs=bf_row[:], start=True, stop=True)
+            nc.vector.tensor_copy(out=bf_b[:], in_=bf_ps[:])
+            for half in range(2):
+                nc.vector.tensor_copy(out=weight_words(wfg, half), in_=interleaved(wf_ps[half]))
             nc.vector.tensor_copy(out=gb[:, 0:4], in_=g_raw[:])
             nc.vector.tensor_copy(out=gb[:, 4:8], in_=b_raw[:])
-            nc.vector.quantize_mx(out=wfc[:].bitcast(FP8X4), scales=wfs[:], in_=wfg[:].rearrange("p c t -> p (c t)"))
 
-        def st_th(pr):
+        def prep_wf_quantise():
+            nc.vector.quantize_mx(out=wfc[:].bitcast(FP8X4), scales=wfs[:], in_=wfg[:])
+
+        S = {}
+
+        def st_xp(q):
+            for j in range(QT):
+                xp = work.tile([P, DIM], F32, tag="xp", bufs=4, name="xp")
+                S[("xp", q, j)] = xp
+                nc.gpsimd.tensor_tensor(out=xp[:].rearrange("p (t m) -> p t m", t=4),
+                                        in0=x_tiles[q // 2][:, (q % 2) * QT + j, :].rearrange("p (m t) -> p t m", t=4),
+                                        in1=bo_p[:].rearrange("p (t m) -> p t m", t=4), op=ALU.add)
+
+        def st_th(q, half):
             ht = psum.tile([P, 2, 2, P], F32, tag="ht", name="ht")
-            S[("ht", pr)] = ht
+            S[("ht", q, half)] = ht
             for jj in range(2):
-                hsrc = h_tiles[pr // 4][:, (pr % 4) * 2 + jj, :]
+                src = h_tiles[q // 2][:, (q % 2) * QT + 2 * half + jj, :].bitcast(F32)
                 for u in range(2):
-                    nc.tensor.transpose(ht[:, jj, u, :], hsrc.bitcast(F32)[:, u::2], ident_f[:])
+                    nc.tensor.transpose(ht[:, jj, u, :], src[:, u::2], ident_f[:])
 
-        def st_a(pr):
-            q = pr // 2
-            if pr % 2 == 0:
-                hg_new = work.tile([P, 4 * DIM], BF16, tag="hg", bufs=4, align_bytes=64, name="hg")
-                S[("hg", q)] = hg_new
-            hg = S[("hg", q)]
-            j0 = (pr % 2) * 2
-            nc.scalar.copy(out=hg[:].bitcast(F32).rearrange("p (j r u) -> p j r u", j=4, u=2)[:, j0:j0 + 2, :, :],
-                           in_=S[("ht", pr)][:].rearrange("p j u r -> p j r u"))
+        def st_a(q, half):
+            if half == 0:
+                hg = work.tile([P, QT * DIM], BF16, tag="hg", bufs=3, align_bytes=64, name="hg")
+                S[("hg", q)] = hg
+            nc.scalar.copy(out=S[("hg", q)][:].bitcast(F32).rearrange("p (j r u) -> p j r u", j=QT, u=2)[:, 2 * half:2 * half + 2, :, :],
+                           in_=S[("ht", q, half)][:].rearrange("p j u r -> p j r u"))
 
         def st_qh(q):
-            hc = work.tile([P, 4 * P], U32, tag="hc", bufs=3, align_bytes=64, name="hc")
-            hs = work.tile([P, 4 * P], U8, tag="hs", bufs=3, align_bytes=64, name="hs")
+            hc = work.tile([P, QT * P], U32, tag="hc", bufs=3, align_bytes=64, name="hc")
+            hs = work.tile([P, QT * P], U8, tag="hs", bufs=3, align_bytes=64, name="hs")
             S[("hc", q)] = (hc, hs)
             nc.vector.quantize_mx(out=hc[:].bitcast(FP8X4), scales=hs[:], in_=S[("hg", q)][:])
 
-        def st_mx1(pr):
-            hc, hs = S[("hc", pr // 2)]
-            for jj in range(2):
-                c0 = ((pr % 2) * 2 + jj) * P
-                p1 = psum.tile([P, DIM], F32, tag="p1", name="p1")
-                S[("p1", pr, jj)] = p1
-                nc.tensor.matmul_mx(out=p1[:], lhsT=hc[:, c0:c0 + P].bitcast(FP8X4), lhsT_scale=hs[:, c0:c0 + P],
-                                    rhs=woc[:].bitcast(FP8X4), rhs_scale=wos[:], start=True, stop=True)
+        def st_mx1(q, j):
+            hc, hs = S[("hc", q)]
+            p1 = psum.tile([P, DIM], F32, tag="p1", name="p1")
+            S[("p1", q, j)] = p1
+            nc.tensor.matmul_mx(out=p1[:], lhsT=hc[:, j * P:(j + 1) * P].bitcast(FP8X4), lhsT_scale=hs[:, j * P:(j + 1) * P],
+                                rhs=woc[:].bitcast(FP8X4), rhs_scale=wos[:], start=True, stop=True)
 
-        def st_c(pr):
-            q = pr // 2
-            if pr % 2 == 0:
-                sums_new = stats.tile([P, 4], F32, tag="sums", name="sums")
-                S[("sums", q)] = sums_new
-            sums = S[("sums", q)]
-            for jj in range(2):
-                j = (pr % 2) * 2 + jj
-                y = work.tile([P, DIM], F32, tag="y", bufs=20, name="y")
-                S[("y", pr, jj)] = y
-                nc.vector.scalar_tensor_tensor(out=y[:], in0=S[("p1", pr, jj)][:], scalar=0.0, in1=S[("xp", q)][:, j, :],
-                                               op0=ALU.add, op1=ALU.add, accum_out=sums[:, j:j + 1])
+        def st_c(q, j):
+            if j == 0:
+                sums = stats.tile([P, QT], F32, tag="sums", name="sums")
+                S[("sums", q)] = sums
+            y = work.tile([P, DIM], F32, tag="y", bufs=12, name="y")
+            S[("y", q, j)] = y
+            nc.vector.scalar_tensor_tensor(out=y[:], in0=S[("p1", q, j)][:], scalar=0.0, in1=S[("xp", q, j)][:],
+                                           op0=ALU.add, op1=ALU.add, accum_out=S[("sums", q)][:, j:j + 1])
 
         def st_negmu(q):
-            negmu = stats.tile([P, 4], F32, tag="negmu", name="negmu")
+            negmu = stats.tile([P, QT], F32, tag="negmu", name="negmu")
             S[("negmu", q)] = negmu
-            nc.gpsimd.tensor_scalar(out=negmu[:], in0=S[("sums", q)][:], scalar1=-1.0 / DIM, scalar2=0.0, op0=ALU.mult, op1=ALU.add)
+            nc.vector.tensor_scalar(out=negmu[:], in0=S[("sums", q)][:], scalar1=-1.0 / DIM, scalar2=None, op0=ALU.mult)
 
-        def st_d(pr):
-            q = pr // 2
-            if pr % 2 == 0:
-                ssq_new = stats.tile([P, 4], F32, tag="ssq", name="ssq")
-                S[("ssq", q)] = ssq_new
-            ssq = S[("ssq", q)]
-            negmu = S[("negmu", q)]
-            for jj in range(2):
-                j = (pr % 2) * 2 + jj
+        def st_d(q):
+            ssq = stats.tile([P, QT], F32, tag="ssq", name="ssq")
+            S[("ssq", q)] = ssq
+            for j in range(QT):
                 junk = work.tile([P, DIM], BF16, tag="junk", name="junk")
-                nc.scalar.activation(out=junk[:], in_=S[("y", pr, jj)][:], func=ACT.Square, bias=negmu[:, j:j + 1], scale=1.0,
+                nc.scalar.activation(out=junk[:], in_=S[("y", q, j)][:], func=ACT.Square, bias=S[("negmu", q)][:, j:j + 1], scale=1.0,
                                      accum_out=ssq[:, j:j + 1])
 
-        def st_ars(q):
-            rstd = stats.tile([P, 4], F32, tag="rstd", name="rstd")
+        def st_rstd(q):
+            rstd = stats.tile([P, QT], F32, tag="rstd", name="rstd")
             S[("rstd", q)] = rstd
             nc.scalar.activation(out=rstd[:], in_=S[("ssq", q)][:], func=ACT.Abs_reciprocal_sqrt, bias=eps_t[:, 0:1], scale=1.0 / DIM)
 
         def st_nmr(q):
-            nmr = stats.tile([P, 4], F32, tag="nmr", name="nmr")
+            nmr = stats.tile([P, QT], F32, tag="nmr", name="nmr")
             S[("nmr", q)] = nmr
-            nc.gpsimd.tensor_tensor(out=nmr[:], in0=S[("negmu", q)][:], in1=S[("rstd", q)][:], op=ALU.mult)
+            nc.vector.tensor_tensor(out=nmr[:], in0=S[("negmu", q)][:], in1=S[("rstd", q)][:], op=ALU.mult)
 
-        def st_e(pr):
-            q = pr // 2
-            for jj in range(2):
-                j = (pr % 2) * 2 + jj
-                y = S[("y", pr, jj)]
+        def st_e(q):
+            for j in range(QT):
+                y = S[("y", q, j)]
+                if q < 2:
+                    nc.vector.tensor_scalar(out=y[:], in0=y[:], scalar1=S[("negmu", q)][:, j:j + 1], scalar2=S[("rstd", q)][:, j:j + 1],
+                                            op0=ALU.add, op1=ALU.mult)
+                    continue
                 nc.scalar.activation(out=y[:], in_=y[:], func=ACT.Identity, bias=S[("nmr", q)][:, j:j + 1], scale=S[("rstd", q)][:, j:j + 1])
 
-        def st_tz(s):
-            q = s // 2
-            for tt in range(2):
-                t = 2 * (s % 2) + tt
-                zt = psum.tile([P, 4, P], F32, tag="zt", name="zt")
-                S[("zt", q, t)] = zt
-                for j in range(4):
-                    nc.tensor.transpose(zt[:, j, :], S[("y", 2 * q + j // 2, j % 2)][:, t::4], ident_f[:])
+        def st_tz(q, t):
+            zt = psum.tile([P, QT, P], F32, tag="zt", name="zt")
+            S[("zt", q, t)] = zt
+            for j in range(QT):
+                nc.tensor.transpose(zt[:, j, :], S[("y", q, j)][:, t * P:(t + 1) * P], ident_f[:])
 
-        def st_f(s):
-            q = s // 2
-            if s % 2 == 0:
-                planes_new = work.tile([P, 4, 4 * P], BF16, tag="planes", bufs=3, name="planes")
-                S[("planes", q)] = planes_new
-            planes = S[("planes", q)]
-            for tt in range(2):
-                t = 2 * (s % 2) + tt
-                nc.scalar.activation(out=planes[:, t, :], in_=S[("zt", q, t)][:].rearrange("p j r -> p (j r)"),
-                                     func=ACT.Identity, bias=gb[:, 4 + t:5 + t], scale=gb[:, t:t + 1])
+        def st_f(q, t):
+            if t == 0:
+                planes = work.tile([P, 4, QT * P], BF16, tag="planes", bufs=3, name="planes")
+                S[("planes", q)] = planes
+            nc.scalar.activation(out=S[("planes", q)][:, t, :], in_=S[("zt", q, t)][:].rearrange("p j r -> p (j r)"),
+                                 func=ACT.Identity, bias=gb[:, 4 + t:5 + t], scale=gb[:, t:t + 1])
 
         def st_f2(q):
-            xg = work.tile([P, 4 * P, 4], BF16, tag="xg", bufs=2, align_bytes=64, name="xg")
+            xg = work.tile([P, QT * P, 4], BF16, tag="xg", bufs=2, align_bytes=64, name="xg")
             S[("xg", q)] = xg
             nc.vector.tensor_copy(out=xg[:].rearrange("p (c i) t -> p c t i", i=4),
                                   in_=S[("planes", q)][:].rearrange("p t (c i) -> p c t i", i=4))
 
         def st_qx(q):
-            xc = work.tile([P, 4 * P], U32, tag="xc", bufs=3, align_bytes=64, name="xc")
-            xs = work.tile([P, 4 * P], U8, tag="xs", bufs=3, align_bytes=64, name="xs")
+            xc = work.tile([P, QT * P], U32, tag="xc", bufs=3, align_bytes=64, name="xc")
+            xs = work.tile([P, QT * P], U8, tag="xs", bufs=3, align_bytes=64, name="xs")
             S[("xc", q)] = (xc, xs)
             nc.vector.quantize_mx(out=xc[:].bitcast(FP8X4), scales=xs[:], in_=S[("xg", q)][:].rearrange("p c t -> p (c t)"))
 
-        def st_mx2(pr):
-            xc, xs = S[("xc", pr // 2)]
-            for jj in range(2):
-                c0 = ((pr % 2) * 2 + jj) * P
-                p2 = psum.tile([P, DIM], F32, tag="p2", name="p2")
-                S[("p2", pr, jj)] = p2
-                nc.tensor.matmul_mx(out=p2[:], lhsT=xc[:, c0:c0 + P].bitcast(FP8X4), lhsT_scale=xs[:, c0:c0 + P],
-                                    rhs=wfc[:].bitcast(FP8X4), rhs_scale=wfs[:], start=True, stop=True)
+        def st_mx2(q, j):
+            xc, xs = S[("xc", q)]
+            p2 = psum.tile([P, DIM], F32, tag="p2", name="p2")
+            S[("p2", q, j)] = p2
+            nc.tensor.matmul_mx(out=p2[:], lhsT=xc[:, j * P:(j + 1) * P].bitcast(FP8X4), lhsT_scale=xs[:, j * P:(j + 1) * P],
+                                rhs=wfc[:].bitcast(FP8X4), rhs_scale=wfs[:], start=True, stop=True)
 
-        def st_h1(pr):
-            q = pr // 2
-            if pr % 2 == 0:
-                o_new = work.tile([P, 4, DIM], F32, tag="o", bufs=3, name="o")
-                S[("o", q)] = o_new
-            o = S[("o", q)]
-            for jj in range(2):
-                nc.vector.tensor_tensor(out=o[:, (pr % 2) * 2 + jj, :], in0=S[("p2", pr, jj)][:], in1=bf_b[:], op=ALU.add)
+        def st_h(q, j):
+            if j == 0:
+                o = work.tile([P, QT, DIM], F32, tag="o", bufs=3, name="o")
+                S[("o", q)] = o
+            nc.vector.tensor_tensor(out=S[("o", q)][:, j, :], in0=S[("p2", q, j)][:], in1=bf_b[:], op=ALU.add)
 
         def st_relu(q):
             o = S[("o", q)]
-            j0 = (q % 2) * 4
-            if q == NQUAD - 1:
+            j0 = (q % 2) * QT
+            if q == NQ - 1:
+                for j in range(QT):
+                    nc.scalar.activation(out=o[:, j, :], in_=o[:, j, :], func=ACT.Relu)
+                    nc.sync.dma_start(out=ov[q // 2][:, j0 + j, :], in_=o[:, j, :])
                 return
-            if q % 2 == 1:
-                nc.vector.tensor_scalar(out=o[:], in0=o[:], scalar1=0.0, scalar2=None, op0=ALU.max)
-            else:
+            if q >= NQ - 3:
                 nc.scalar.activation(out=o[:], in_=o[:], func=ACT.Relu)
-            nc.sync.dma_start(out=ov[q // 2][:, j0:j0 + 4, :], in_=o[:])
-
-        def st_relu_last(pr):
-            if pr // 2 != NQUAD - 1:
-                return
-            o = S[("o", pr // 2)]
-            j1 = (pr % 2) * 2
-            if pr % 2 == 0:
-                nc.scalar.activation(out=o[:, j1:j1 + 2, :], in_=o[:, j1:j1 + 2, :], func=ACT.Relu)
-                nc.sync.dma_start(out=ov[pr // 4][:, 4 + j1:4 + j1 + 2, :], in_=o[:, j1:j1 + 2, :])
             else:
-                nc.scalar.activation(out=o[:, 2, :], in_=o[:, 2, :], func=ACT.Relu)
-                nc.sync.dma_start(out=ov[pr // 4][:, 6, :], in_=o[:, 2, :])
-                nc.vector.tensor_scalar(out=o[:, 3, :], in0=o[:, 3, :], scalar1=0.0, scalar2=None, op0=ALU.max)
-                nc.sync.dma_start(out=ov[pr // 4][:, 7, :], in_=o[:, 3, :])
+                nc.vector.tensor_scalar(out=o[:], in0=o[:], scalar1=0.0, scalar2=None, op0=ALU.max)
+            nc.sync.dma_start(out=ov[q // 2][:, j0:j0 + QT, :], in_=o[:])
 
-        def on(fn, pr):
-            if 0 <= pr < NPAIR:
-                fn(pr)
+        def on(fn, q, *rest):
+            if 0 <= q < NQ:
+                fn(q, *rest)
 
-        def onq(fn, m):
-            if m % 2 == 0 and 0 <= m // 2 < NQUAD:
-                fn(m // 2)
-
-        for n in range(NPAIR + 26):
-            if n % 4 == 3 and n >= 7 and n // 4 + 2 < NCH:
-                load_h(n // 4 + 2, 1)
-                load_x(n // 4 + 2, 1)
-            if n == 2:
+        for s in range(-2, NQ + 3):
+            on(st_c, s, 0)
+            on(st_mx1, s, 2)
+            on(st_c, s, 1)
+            on(st_mx1, s, 3)
+            on(st_c, s, 2)
+            on(st_c, s, 3)
+            if s in (1, 2):
+                st_e(s - 1)
+            on(st_mx2, s - 3, 0)
+            on(st_mx2, s - 3, 1)
+            if s == 1:
+                prep_wf_copies()
+            on(st_h, s - 3, 0)
+            on(st_negmu, s)
+            on(st_mx2, s - 3, 2)
+            on(st_h, s - 3, 1)
+            on(st_mx2, s - 3, 3)
+            on(st_h, s - 3, 2)
+            on(st_h, s - 3, 3)
+            on(st_tz, s - 1, 0)
+            on(st_tz, s - 1, 1)
+            on(st_d, s)
+            on(st_xp, s + 1)
+            on(st_th, s + 2, 0)
+            on(st_th, s + 2, 1)
+            on(st_qh, s + 1)
+            on(st_f, s - 1, 0)
+            on(st_rstd, s)
+            on(st_mx1, s + 1, 0)
+            on(st_tz, s - 1, 2)
+            on(st_f, s - 1, 1)
+            on(st_mx1, s + 1, 1)
+            on(st_tz, s - 1, 3)
+            on(st_f, s - 1, 2)
+            on(st_f, s - 1, 3)
+            on(st_f2, s - 2)
+            on(st_relu, s - 3)
+            on(st_qx, s - 2)
+            if s >= 2:
+                on(st_nmr, s)
+            on(st_a, s + 2, 0)
+            on(st_a, s + 2, 1)
+            if s >= 2:
+                on(st_e, s)
+            if s == 0:
                 prep_wf_transposes()
-            if n == 3:
-                st_xp(2)
-            if n == 5:
+            if s == 1:
                 prep_wf_quantise()
-            if n >= 10:
-                onq(st_xp, n - 4)
-            onq(st_qx, n - 20)
-            on(st_c, n - 7)
-            on(st_mx1, n - 6)
-            onq(st_qh, n - 5)
-            on(st_h1, n - 22)
-            on(st_mx2, n - 21)
-            onq(st_negmu, n - 8)
-            on(st_e, n - 13)
-            on(st_a, n - 1)
-            on(st_th, n)
-            on(st_d, n - 10)
-            on(st_f, n - 15)
-            on(st_tz, n - 14)
-            onq(st_ars, n - 11)
-            onq(st_nmr, n - 11)
-            onq(st_f2, n - 19)
-            on(st_relu_last, n - 23)
-            onq(st_relu, n - 25)
+            if s % 2 == 0 and 0 <= s and (s + 6) // 2 < NCH:
+                load_part(h_tiles, hv, "h", (s + 6) // 2, 0, CH)
+                load_part(x_tiles, xv, "x", (s + 6) // 2, 0, CH)

@@ -34,7 +34,7 @@ def tile_l1regressionmoeactionhead_pc_t_kernel(tc, h_attn, x, W_o, b_o, W_ffn, b
         loads = ctx.enter_context(tc.tile_pool(name="loads", bufs=3))
         work = ctx.enter_context(tc.tile_pool(name="work", bufs=2))
         stats = ctx.enter_context(tc.tile_pool(name="stats", bufs=4))
-        psum = ctx.enter_context(tc.psum_pool(name="psum", bufs=2))
+        psum = ctx.enter_context(tc.psum_pool(name="psum", bufs=4))
         ctx.enter_context(tc.manual_schedule(engines={ENG.PE, ENG.Activation, ENG.DVE, ENG.Pool}))
 
         h_tiles = {}
@@ -47,7 +47,7 @@ def tile_l1regressionmoeactionhead_pc_t_kernel(tc, h_attn, x, W_o, b_o, W_ffn, b
             nc.sync.dma_start(out=tiles[c][:, j0:j1, :], in_=view[c][:, j0:j1, :])
 
         wo_sb = const.tile([P, 4, DIM], BF16)
-        nc.sync.dma_start(out=wo_sb[:], in_=W_o.rearrange("(p t) k -> p t k", t=4))
+        nc.sync.dma_start(out=wo_sb[:], in_=W_o.rearrange("(r p) k -> p r k", p=P))
         load_part(h_tiles, hv, "h", 0, 0, 4)
         load_part(x_tiles, xv, "x", 0, 0, 4)
         load_part(h_tiles, hv, "h", 0, 4, 8)
@@ -78,12 +78,12 @@ def tile_l1regressionmoeactionhead_pc_t_kernel(tc, h_attn, x, W_o, b_o, W_ffn, b
         warm = const.tile([P, 1], F32)
         nc.scalar.activation(out=warm[:], in_=eps_t[:], func=ACT.Abs_reciprocal_sqrt)
 
-        bo_p = const.tile([P, DIM], BF16)
+        bo_b = const.tile([P, DIM], BF16)
         bf_b = const.tile([P, DIM], BF16)
         gb = const.tile([P, 8], F32)
 
-        def weight_transposes(w_sb, half, tag):
-            wt = psum.tile([P, 4, P], F32, tag=tag, name="wt")
+        def weight_transposes(w_sb, half):
+            wt = psum.tile([P, 4, P], F32, tag="tr", name="wt")
             for rr in range(2):
                 for u in range(2):
                     nc.tensor.transpose(wt[:, 2 * rr + u, :], w_sb[:, 2 * half + rr, :].bitcast(F32)[:, u::2], ident_f[:])
@@ -102,23 +102,23 @@ def tile_l1regressionmoeactionhead_pc_t_kernel(tc, h_attn, x, W_o, b_o, W_ffn, b
         wfc = const.tile([P, DIM], U32, align_bytes=64)
         wfs = const.tile([P, DIM], U8, align_bytes=64)
 
-        wt_a = weight_transposes(wo_sb, 0, "zt")
-        wt_b = weight_transposes(wo_sb, 1, "zt")
-        bo_ps = psum.tile([P, DIM], F32, tag="p2", name="bo_ps")
+        wt_a = weight_transposes(wo_sb, 0)
+        wt_b = weight_transposes(wo_sb, 1)
+        bo_ps = psum.tile([P, DIM], F32, tag="mm", name="bo_ps")
         nc.tensor.matmul(bo_ps[:], lhsT=ones[:], rhs=bo_row[:], start=True, stop=True)
         nc.vector.tensor_copy(out=weight_words(wog, 0), in_=interleaved(wt_a))
         nc.scalar.copy(out=weight_words(wog, 1), in_=interleaved(wt_b))
-        nc.vector.tensor_copy(out=bo_p[:].rearrange("p (t m) -> p t m", t=4), in_=bo_ps[:].rearrange("p (m t) -> p t m", t=4))
+        nc.vector.tensor_copy(out=bo_b[:], in_=bo_ps[:])
         nc.vector.quantize_mx(out=woc[:].bitcast(FP8X4), scales=wos[:], in_=wog[:])
 
         wf_ps = []
 
         def prep_wf_transposes():
             for half in range(2):
-                wf_ps.append(weight_transposes(wf_sb, half, "zt"))
+                wf_ps.append(weight_transposes(wf_sb, half))
 
         def prep_wf_copies():
-            bf_ps = psum.tile([P, DIM], F32, tag="p2", name="bf_ps")
+            bf_ps = psum.tile([P, DIM], F32, tag="mm", name="bf_ps")
             nc.tensor.matmul(bf_ps[:], lhsT=ones[:], rhs=bf_row[:], start=True, stop=True)
             nc.vector.tensor_copy(out=bf_b[:], in_=bf_ps[:])
             for half in range(2):
@@ -135,24 +135,23 @@ def tile_l1regressionmoeactionhead_pc_t_kernel(tc, h_attn, x, W_o, b_o, W_ffn, b
             for j in range(QT):
                 xp = work.tile([P, DIM], F32, tag="xp", bufs=4, name="xp")
                 S[("xp", q, j)] = xp
-                nc.gpsimd.tensor_tensor(out=xp[:].rearrange("p (t m) -> p t m", t=4),
-                                        in0=x_tiles[q // 2][:, (q % 2) * QT + j, :].rearrange("p (m t) -> p t m", t=4),
-                                        in1=bo_p[:].rearrange("p (t m) -> p t m", t=4), op=ALU.add)
+                engine = nc.gpsimd if j < 3 else nc.vector
+                engine.tensor_tensor(out=xp[:], in0=x_tiles[q // 2][:, (q % 2) * QT + j, :], in1=bo_b[:], op=ALU.add)
 
         def st_th(q, half):
-            ht = psum.tile([P, 2, 2, P], F32, tag="ht", name="ht")
+            ht = psum.tile([P, 4, P], F32, tag="tr", name="ht")
             S[("ht", q, half)] = ht
             for jj in range(2):
                 src = h_tiles[q // 2][:, (q % 2) * QT + 2 * half + jj, :].bitcast(F32)
                 for u in range(2):
-                    nc.tensor.transpose(ht[:, jj, u, :], src[:, u::2], ident_f[:])
+                    nc.tensor.transpose(ht[:, 2 * jj + u, :], src[:, u::2], ident_f[:])
 
         def st_a(q, half):
             if half == 0:
                 hg = work.tile([P, QT * DIM], BF16, tag="hg", bufs=3, align_bytes=64, name="hg")
                 S[("hg", q)] = hg
             nc.scalar.copy(out=S[("hg", q)][:].bitcast(F32).rearrange("p (j r u) -> p j r u", j=QT, u=2)[:, 2 * half:2 * half + 2, :, :],
-                           in_=S[("ht", q, half)][:].rearrange("p j u r -> p j r u"))
+                           in_=S[("ht", q, half)][:].rearrange("p (j u) r -> p j r u", u=2))
 
         def st_qh(q):
             hc = work.tile([P, QT * P], U32, tag="hc", bufs=3, align_bytes=64, name="hc")
@@ -162,7 +161,7 @@ def tile_l1regressionmoeactionhead_pc_t_kernel(tc, h_attn, x, W_o, b_o, W_ffn, b
 
         def st_mx1(q, j):
             hc, hs = S[("hc", q)]
-            p1 = psum.tile([P, DIM], F32, tag="p1", name="p1")
+            p1 = psum.tile([P, DIM], F32, tag="mm", name="p1")
             S[("p1", q, j)] = p1
             nc.tensor.matmul_mx(out=p1[:], lhsT=hc[:, j * P:(j + 1) * P].bitcast(FP8X4), lhsT_scale=hs[:, j * P:(j + 1) * P],
                                 rhs=woc[:].bitcast(FP8X4), rhs_scale=wos[:], start=True, stop=True)
@@ -209,10 +208,10 @@ def tile_l1regressionmoeactionhead_pc_t_kernel(tc, h_attn, x, W_o, b_o, W_ffn, b
                 nc.scalar.activation(out=y[:], in_=y[:], func=ACT.Identity, bias=S[("nmr", q)][:, j:j + 1], scale=S[("rstd", q)][:, j:j + 1])
 
         def st_tz(q, t):
-            zt = psum.tile([P, QT, P], F32, tag="zt", name="zt")
+            zt = psum.tile([P, QT, P], F32, tag="tr", name="zt")
             S[("zt", q, t)] = zt
             for j in range(QT):
-                nc.tensor.transpose(zt[:, j, :], S[("y", q, j)][:, t * P:(t + 1) * P], ident_f[:])
+                nc.tensor.transpose(zt[:, j, :], S[("y", q, j)][:, t::4], ident_f[:])
 
         def st_f(q, t):
             if t == 0:
@@ -235,7 +234,7 @@ def tile_l1regressionmoeactionhead_pc_t_kernel(tc, h_attn, x, W_o, b_o, W_ffn, b
 
         def st_mx2(q, j):
             xc, xs = S[("xc", q)]
-            p2 = psum.tile([P, DIM], F32, tag="p2", name="p2")
+            p2 = psum.tile([P, DIM], F32, tag="mm", name="p2")
             S[("p2", q, j)] = p2
             nc.tensor.matmul_mx(out=p2[:], lhsT=xc[:, j * P:(j + 1) * P].bitcast(FP8X4), lhsT_scale=xs[:, j * P:(j + 1) * P],
                                 rhs=wfc[:].bitcast(FP8X4), rhs_scale=wfs[:], start=True, stop=True)
@@ -264,55 +263,56 @@ def tile_l1regressionmoeactionhead_pc_t_kernel(tc, h_attn, x, W_o, b_o, W_ffn, b
             if 0 <= q < NQ:
                 fn(q, *rest)
 
-        for s in range(-2, NQ + 3):
-            on(st_c, s, 0)
-            on(st_mx1, s, 2)
-            on(st_c, s, 1)
-            on(st_mx1, s, 3)
-            on(st_c, s, 2)
-            on(st_c, s, 3)
+        for half in range(2):
+            st_th(0, half)
+        for half in range(2):
+            st_a(0, half)
+        st_xp(0)
+        st_qh(0)
+        for j in range(QT):
+            st_mx1(0, j)
+        for half in range(2):
+            st_th(1, half)
+            st_a(1, half)
+        for s in range(NQ + 3):
+            for half in range(2):
+                for j in range(2 * half, 2 * half + 2):
+                    on(st_c, s, j)
+                for j in range(2 * half, 2 * half + 2):
+                    on(st_mx2, s - 3, j)
             if s in (1, 2):
                 st_e(s - 1)
-            on(st_mx2, s - 3, 0)
-            on(st_mx2, s - 3, 1)
-            if s == 1:
-                prep_wf_copies()
             on(st_h, s - 3, 0)
             on(st_negmu, s)
-            on(st_mx2, s - 3, 2)
-            on(st_h, s - 3, 1)
-            on(st_mx2, s - 3, 3)
-            on(st_h, s - 3, 2)
-            on(st_h, s - 3, 3)
-            on(st_tz, s - 1, 0)
-            on(st_tz, s - 1, 1)
+            for j in range(1, QT):
+                on(st_h, s - 3, j)
+            if s == 0:
+                prep_wf_transposes()
+            if s == 1:
+                prep_wf_copies()
             on(st_d, s)
+            for t in range(4):
+                on(st_tz, s - 1, t)
             on(st_xp, s + 1)
-            on(st_th, s + 2, 0)
-            on(st_th, s + 2, 1)
             on(st_qh, s + 1)
+            if s == 1:
+                prep_wf_quantise()
             on(st_f, s - 1, 0)
             on(st_rstd, s)
-            on(st_mx1, s + 1, 0)
-            on(st_tz, s - 1, 2)
-            on(st_f, s - 1, 1)
-            on(st_mx1, s + 1, 1)
-            on(st_tz, s - 1, 3)
-            on(st_f, s - 1, 2)
-            on(st_f, s - 1, 3)
+            for t in range(1, 4):
+                on(st_f, s - 1, t)
+            for j in range(QT):
+                on(st_mx1, s + 1, j)
+            for half in range(2):
+                on(st_th, s + 2, half)
+            for half in range(2):
+                on(st_a, s + 2, half)
             on(st_f2, s - 2)
             on(st_relu, s - 3)
             on(st_qx, s - 2)
             if s >= 2:
                 on(st_nmr, s)
-            on(st_a, s + 2, 0)
-            on(st_a, s + 2, 1)
-            if s >= 2:
                 on(st_e, s)
-            if s == 0:
-                prep_wf_transposes()
-            if s == 1:
-                prep_wf_quantise()
-            if s % 2 == 0 and 0 <= s and (s + 6) // 2 < NCH:
+            if s % 2 == 0 and (s + 6) // 2 < NCH:
                 load_part(h_tiles, hv, "h", (s + 6) // 2, 0, CH)
                 load_part(x_tiles, xv, "x", (s + 6) // 2, 0, CH)

@@ -19,6 +19,7 @@ CH = 8
 NCH = TOKENS // (P * CH)
 QT = 4
 NQ = TOKENS // (P * QT)
+EDGE = (0, 1, NQ - 1)
 EPS = 1e-5
 FLOPS = 2 * 2 * TOKENS * DIM * DIM
 
@@ -48,6 +49,9 @@ def tile_l1regressionmoeactionhead_pc_t_kernel(tc, h_attn, x, W_o, b_o, W_ffn, b
 
         wo_sb = const.tile([P, 4, DIM], BF16)
         nc.sync.dma_start(out=wo_sb[:], in_=W_o.rearrange("(r p) k -> p r k", p=P))
+        bo_row = const.tile([P, DIM], BF16)
+        nc.vector.memset(bo_row[:], 0.0)
+        nc.sync.dma_start(out=bo_row[0:1, :], in_=b_o.unsqueeze(0))
         load_part(h_tiles, hv, "h", 0, 0, 4)
         load_part(x_tiles, xv, "x", 0, 0, 4)
         load_part(h_tiles, hv, "h", 0, 4, 8)
@@ -58,9 +62,6 @@ def tile_l1regressionmoeactionhead_pc_t_kernel(tc, h_attn, x, W_o, b_o, W_ffn, b
             load_part(h_tiles, hv, "h", c, 0, CH)
             load_part(x_tiles, xv, "x", c, 0, CH)
 
-        bo_row = const.tile([P, DIM], BF16)
-        nc.vector.memset(bo_row[:], 0.0)
-        nc.scalar.dma_start(out=bo_row[0:1, :], in_=b_o.unsqueeze(0))
         bf_row = const.tile([P, DIM], BF16)
         nc.vector.memset(bf_row[:], 0.0)
         nc.scalar.dma_start(out=bf_row[0:1, :], in_=b_ffn.unsqueeze(0))
@@ -104,11 +105,8 @@ def tile_l1regressionmoeactionhead_pc_t_kernel(tc, h_attn, x, W_o, b_o, W_ffn, b
 
         wt_a = weight_transposes(wo_sb, 0)
         wt_b = weight_transposes(wo_sb, 1)
-        bo_ps = psum.tile([P, DIM], F32, tag="mm", name="bo_ps")
-        nc.tensor.matmul(bo_ps[:], lhsT=ones[:], rhs=bo_row[:], start=True, stop=True)
         nc.vector.tensor_copy(out=weight_words(wog, 0), in_=interleaved(wt_a))
         nc.scalar.copy(out=weight_words(wog, 1), in_=interleaved(wt_b))
-        nc.vector.tensor_copy(out=bo_b[:], in_=bo_ps[:])
         nc.vector.quantize_mx(out=woc[:].bitcast(FP8X4), scales=wos[:], in_=wog[:])
 
         wf_ps = []
@@ -135,8 +133,15 @@ def tile_l1regressionmoeactionhead_pc_t_kernel(tc, h_attn, x, W_o, b_o, W_ffn, b
             for j in range(QT):
                 xp = work.tile([P, DIM], F32, tag="xp", bufs=4, name="xp")
                 S[("xp", q, j)] = xp
-                engine = nc.gpsimd if j < 3 else nc.vector
-                engine.tensor_tensor(out=xp[:], in0=x_tiles[q // 2][:, (q % 2) * QT + j, :], in1=bo_b[:], op=ALU.add)
+                src = x_tiles[q // 2][:, (q % 2) * QT + j, :]
+                if q == 0:
+                    split = DIM * (1 - j % 2)
+                else:
+                    split = DIM if j < 3 else DIM // 2
+                if split > 0:
+                    nc.gpsimd.tensor_tensor(out=xp[:, :split], in0=src[:, :split], in1=bo_b[:, :split], op=ALU.add)
+                if split < DIM:
+                    nc.vector.tensor_tensor(out=xp[:, split:], in0=src[:, split:], in1=bo_b[:, split:], op=ALU.add)
 
         def st_th(q, half):
             ht = psum.tile([P, 4, P], F32, tag="tr", name="ht")
@@ -201,7 +206,7 @@ def tile_l1regressionmoeactionhead_pc_t_kernel(tc, h_attn, x, W_o, b_o, W_ffn, b
         def st_e(q):
             for j in range(QT):
                 y = S[("y", q, j)]
-                if q < 2:
+                if q in EDGE:
                     nc.vector.tensor_scalar(out=y[:], in0=y[:], scalar1=S[("negmu", q)][:, j:j + 1], scalar2=S[("rstd", q)][:, j:j + 1],
                                             op0=ALU.add, op1=ALU.mult)
                     continue
@@ -265,14 +270,18 @@ def tile_l1regressionmoeactionhead_pc_t_kernel(tc, h_attn, x, W_o, b_o, W_ffn, b
 
         for half in range(2):
             st_th(0, half)
+        bo_ps = psum.tile([P, DIM], F32, tag="mm", name="bo_ps")
+        nc.tensor.matmul(bo_ps[:], lhsT=ones[:], rhs=bo_row[:], start=True, stop=True)
         for half in range(2):
             st_a(0, half)
-        st_xp(0)
+        nc.vector.tensor_copy(out=bo_b[:], in_=bo_ps[:])
+        for half in range(2):
+            st_th(1, half)
         st_qh(0)
+        st_xp(0)
         for j in range(QT):
             st_mx1(0, j)
         for half in range(2):
-            st_th(1, half)
             st_a(1, half)
         for s in range(NQ + 3):
             for half in range(2):
@@ -280,12 +289,12 @@ def tile_l1regressionmoeactionhead_pc_t_kernel(tc, h_attn, x, W_o, b_o, W_ffn, b
                     on(st_c, s, j)
                 for j in range(2 * half, 2 * half + 2):
                     on(st_mx2, s - 3, j)
-            if s in (1, 2):
-                st_e(s - 1)
             on(st_h, s - 3, 0)
             on(st_negmu, s)
             for j in range(1, QT):
                 on(st_h, s - 3, j)
+            if s - 1 in EDGE:
+                st_e(s - 1)
             if s == 0:
                 prep_wf_transposes()
             if s == 1:
@@ -297,8 +306,11 @@ def tile_l1regressionmoeactionhead_pc_t_kernel(tc, h_attn, x, W_o, b_o, W_ffn, b
             on(st_qh, s + 1)
             if s == 1:
                 prep_wf_quantise()
+            if s == NQ - 1:
+                st_rstd(s)
             on(st_f, s - 1, 0)
-            on(st_rstd, s)
+            if s < NQ - 1:
+                st_rstd(s)
             for t in range(1, 4):
                 on(st_f, s - 1, t)
             for j in range(QT):
@@ -310,7 +322,7 @@ def tile_l1regressionmoeactionhead_pc_t_kernel(tc, h_attn, x, W_o, b_o, W_ffn, b
             on(st_f2, s - 2)
             on(st_relu, s - 3)
             on(st_qx, s - 2)
-            if s >= 2:
+            if s not in EDGE:
                 on(st_nmr, s)
                 on(st_e, s)
             if s % 2 == 0 and (s + 6) // 2 < NCH:

@@ -131,7 +131,7 @@ def tile_l1regressionmoeactionhead_pc_t_kernel(tc, h_attn, x, W_o, b_o, W_ffn, b
 
         def st_xp(q):
             for j in range(QT):
-                xp = work.tile([P, DIM], F32, tag="xp", bufs=4, name="xp")
+                xp = work.tile([P, DIM], F32, tag="xp", bufs=8, name="xp")
                 S[("xp", q, j)] = xp
                 src = x_tiles[q // 2][:, (q % 2) * QT + j, :]
                 if q == 0:
@@ -180,35 +180,30 @@ def tile_l1regressionmoeactionhead_pc_t_kernel(tc, h_attn, x, W_o, b_o, W_ffn, b
             nc.vector.scalar_tensor_tensor(out=y[:], in0=S[("p1", q, j)][:], scalar=0.0, in1=S[("xp", q, j)][:],
                                            op0=ALU.add, op1=ALU.add, accum_out=S[("sums", q)][:, j:j + 1])
 
-        def st_negmu(q):
-            negmu = stats.tile([P, QT], F32, tag="negmu", name="negmu")
-            S[("negmu", q)] = negmu
-            nc.vector.tensor_scalar(out=negmu[:], in0=S[("sums", q)][:], scalar1=-1.0 / DIM, scalar2=None, op0=ALU.mult)
-
         def st_d(q):
             ssq = stats.tile([P, QT], F32, tag="ssq", name="ssq")
             S[("ssq", q)] = ssq
             for j in range(QT):
                 junk = work.tile([P, DIM], BF16, tag="junk", name="junk")
-                nc.scalar.activation(out=junk[:], in_=S[("y", q, j)][:], func=ACT.Square, bias=S[("negmu", q)][:, j:j + 1], scale=1.0,
-                                     accum_out=ssq[:, j:j + 1])
+                nc.scalar.activation(out=junk[:], in_=S[("y", q, j)][:], func=ACT.Square, bias=S[("sums", q)][:, j:j + 1],
+                                     scale=-float(DIM), accum_out=ssq[:, j:j + 1])
 
         def st_rstd(q):
             rstd = stats.tile([P, QT], F32, tag="rstd", name="rstd")
             S[("rstd", q)] = rstd
-            nc.scalar.activation(out=rstd[:], in_=S[("ssq", q)][:], func=ACT.Abs_reciprocal_sqrt, bias=eps_t[:, 0:1], scale=1.0 / DIM)
+            nc.scalar.activation(out=rstd[:], in_=S[("ssq", q)][:], func=ACT.Abs_reciprocal_sqrt, bias=eps_t[:, 0:1], scale=1.0 / DIM ** 3)
 
         def st_nmr(q):
             nmr = stats.tile([P, QT], F32, tag="nmr", name="nmr")
             S[("nmr", q)] = nmr
-            nc.vector.tensor_tensor(out=nmr[:], in0=S[("negmu", q)][:], in1=S[("rstd", q)][:], op=ALU.mult)
+            nc.vector.scalar_tensor_tensor(out=nmr[:], in0=S[("sums", q)][:], scalar=-1.0 / DIM, in1=S[("rstd", q)][:], op0=ALU.mult, op1=ALU.mult)
 
         def st_e(q):
             for j in range(QT):
                 y = S[("y", q, j)]
                 if q in EDGE:
-                    nc.vector.tensor_scalar(out=y[:], in0=y[:], scalar1=S[("negmu", q)][:, j:j + 1], scalar2=S[("rstd", q)][:, j:j + 1],
-                                            op0=ALU.add, op1=ALU.mult)
+                    nc.vector.tensor_scalar(out=y[:], in0=y[:], scalar1=S[("rstd", q)][:, j:j + 1], scalar2=S[("nmr", q)][:, j:j + 1],
+                                            op0=ALU.mult, op1=ALU.add)
                     continue
                 nc.scalar.activation(out=y[:], in_=y[:], func=ACT.Identity, bias=S[("nmr", q)][:, j:j + 1], scale=S[("rstd", q)][:, j:j + 1])
 
@@ -236,6 +231,10 @@ def tile_l1regressionmoeactionhead_pc_t_kernel(tc, h_attn, x, W_o, b_o, W_ffn, b
             xs = work.tile([P, QT * P], U8, tag="xs", bufs=3, align_bytes=64, name="xs")
             S[("xc", q)] = (xc, xs)
             nc.vector.quantize_mx(out=xc[:].bitcast(FP8X4), scales=xs[:], in_=S[("xg", q)][:].rearrange("p c t -> p (c t)"))
+
+        def st_gate(q):
+            gate = stats.tile([P, 1], U32, tag="gate", name="gate")
+            nc.gpsimd.tensor_copy(out=gate[:], in_=S[("xc", q)][0][:, 0:1])
 
         def st_mx2(q, j):
             xc, xs = S[("xc", q)]
@@ -289,11 +288,10 @@ def tile_l1regressionmoeactionhead_pc_t_kernel(tc, h_attn, x, W_o, b_o, W_ffn, b
                     on(st_c, s, j)
                 for j in range(2 * half, 2 * half + 2):
                     on(st_mx2, s - 3, j)
-            on(st_h, s - 3, 0)
-            on(st_negmu, s)
-            for j in range(1, QT):
+            for j in range(QT):
                 on(st_h, s - 3, j)
             if s - 1 in EDGE:
+                st_nmr(s - 1)
                 st_e(s - 1)
             if s == 0:
                 prep_wf_transposes()
@@ -302,6 +300,7 @@ def tile_l1regressionmoeactionhead_pc_t_kernel(tc, h_attn, x, W_o, b_o, W_ffn, b
             on(st_d, s)
             for t in range(4):
                 on(st_tz, s - 1, t)
+            on(st_gate, s - 3)
             on(st_xp, s + 1)
             on(st_qh, s + 1)
             if s == 1:
@@ -321,9 +320,10 @@ def tile_l1regressionmoeactionhead_pc_t_kernel(tc, h_attn, x, W_o, b_o, W_ffn, b
                 on(st_a, s + 2, half)
             on(st_f2, s - 2)
             on(st_relu, s - 3)
-            on(st_qx, s - 2)
             if s not in EDGE:
                 on(st_nmr, s)
+            on(st_qx, s - 2)
+            if s not in EDGE:
                 on(st_e, s)
             if s % 2 == 0 and (s + 6) // 2 < NCH:
                 load_part(h_tiles, hv, "h", (s + 6) // 2, 0, CH)

@@ -19,7 +19,7 @@ CH = 8
 NCH = TOKENS // (P * CH)
 QT = 4
 NQ = TOKENS // (P * QT)
-EDGE = (0, 1, NQ - 1)
+LAG = 3
 EPS = 1e-5
 FLOPS = 2 * 2 * TOKENS * DIM * DIM
 
@@ -79,7 +79,7 @@ def tile_l1regressionmoeactionhead_pc_t_kernel(tc, h_attn, x, W_o, b_o, W_ffn, b
         warm = const.tile([P, 1], F32)
         nc.scalar.activation(out=warm[:], in_=eps_t[:], func=ACT.Abs_reciprocal_sqrt)
 
-        bo_b = const.tile([P, DIM], BF16)
+        bo_b = const.tile([P, QT, DIM], BF16)
         bf_b = const.tile([P, DIM], BF16)
         gb = const.tile([P, 8], F32)
 
@@ -111,14 +111,16 @@ def tile_l1regressionmoeactionhead_pc_t_kernel(tc, h_attn, x, W_o, b_o, W_ffn, b
 
         wf_ps = []
 
+        def prep_bf():
+            bf_ps = psum.tile([P, DIM], F32, tag="mm", name="bf_ps")
+            nc.tensor.matmul(bf_ps[:], lhsT=ones[:], rhs=bf_row[:], start=True, stop=True)
+            nc.vector.tensor_copy(out=bf_b[:], in_=bf_ps[:])
+
         def prep_wf_transposes():
             for half in range(2):
                 wf_ps.append(weight_transposes(wf_sb, half))
 
         def prep_wf_copies():
-            bf_ps = psum.tile([P, DIM], F32, tag="mm", name="bf_ps")
-            nc.tensor.matmul(bf_ps[:], lhsT=ones[:], rhs=bf_row[:], start=True, stop=True)
-            nc.vector.tensor_copy(out=bf_b[:], in_=bf_ps[:])
             for half in range(2):
                 nc.vector.tensor_copy(out=weight_words(wfg, half), in_=interleaved(wf_ps[half]))
             nc.vector.tensor_copy(out=gb[:, 0:4], in_=g_raw[:])
@@ -130,18 +132,17 @@ def tile_l1regressionmoeactionhead_pc_t_kernel(tc, h_attn, x, W_o, b_o, W_ffn, b
         S = {}
 
         def st_xp(q):
+            xp = work.tile([P, QT, DIM], F32, tag="xp", bufs=2, name="xp")
+            S[("xp", q)] = xp
+            j0 = (q % 2) * QT
+            xq = x_tiles[q // 2]
+            if q > LAG:
+                nc.gpsimd.tensor_tensor(out=xp[:].rearrange("p j k -> p (j k)"), in0=xq[:, j0:j0 + QT, :].rearrange("p j k -> p (j k)"),
+                                        in1=bo_b[:].rearrange("p j k -> p (j k)"), op=ALU.add)
+                return
             for j in range(QT):
-                xp = work.tile([P, DIM], F32, tag="xp", bufs=8, name="xp")
-                S[("xp", q, j)] = xp
-                src = x_tiles[q // 2][:, (q % 2) * QT + j, :]
-                if q == 0:
-                    split = DIM * (1 - j % 2)
-                else:
-                    split = DIM if j < 3 else DIM // 2
-                if split > 0:
-                    nc.gpsimd.tensor_tensor(out=xp[:, :split], in0=src[:, :split], in1=bo_b[:, :split], op=ALU.add)
-                if split < DIM:
-                    nc.vector.tensor_tensor(out=xp[:, split:], in0=src[:, split:], in1=bo_b[:, split:], op=ALU.add)
+                engine = nc.gpsimd if q == 0 and j % 2 == 0 else nc.vector
+                engine.tensor_tensor(out=xp[:, j, :], in0=xq[:, j0 + j, :], in1=bo_b[:, 0, :], op=ALU.add)
 
         def st_th(q, half):
             ht = psum.tile([P, 4, P], F32, tag="tr", name="ht")
@@ -177,7 +178,7 @@ def tile_l1regressionmoeactionhead_pc_t_kernel(tc, h_attn, x, W_o, b_o, W_ffn, b
                 S[("sums", q)] = sums
             y = work.tile([P, DIM], F32, tag="y", bufs=12, name="y")
             S[("y", q, j)] = y
-            nc.vector.scalar_tensor_tensor(out=y[:], in0=S[("p1", q, j)][:], scalar=0.0, in1=S[("xp", q, j)][:],
+            nc.vector.scalar_tensor_tensor(out=y[:], in0=S[("p1", q, j)][:], scalar=0.0, in1=S[("xp", q)][:, j, :],
                                            op0=ALU.add, op1=ALU.add, accum_out=S[("sums", q)][:, j:j + 1])
 
         def st_d(q):
@@ -201,10 +202,6 @@ def tile_l1regressionmoeactionhead_pc_t_kernel(tc, h_attn, x, W_o, b_o, W_ffn, b
         def st_e(q):
             for j in range(QT):
                 y = S[("y", q, j)]
-                if q in EDGE:
-                    nc.vector.tensor_scalar(out=y[:], in0=y[:], scalar1=S[("rstd", q)][:, j:j + 1], scalar2=S[("nmr", q)][:, j:j + 1],
-                                            op0=ALU.mult, op1=ALU.add)
-                    continue
                 nc.scalar.activation(out=y[:], in_=y[:], func=ACT.Identity, bias=S[("nmr", q)][:, j:j + 1], scale=S[("rstd", q)][:, j:j + 1])
 
         def st_tz(q, t):
@@ -273,7 +270,7 @@ def tile_l1regressionmoeactionhead_pc_t_kernel(tc, h_attn, x, W_o, b_o, W_ffn, b
         nc.tensor.matmul(bo_ps[:], lhsT=ones[:], rhs=bo_row[:], start=True, stop=True)
         for half in range(2):
             st_a(0, half)
-        nc.vector.tensor_copy(out=bo_b[:], in_=bo_ps[:])
+        nc.vector.tensor_copy(out=bo_b[:, 0, :], in_=bo_ps[:])
         for half in range(2):
             st_th(1, half)
         st_qh(0)
@@ -282,49 +279,102 @@ def tile_l1regressionmoeactionhead_pc_t_kernel(tc, h_attn, x, W_o, b_o, W_ffn, b
             st_mx1(0, j)
         for half in range(2):
             st_a(1, half)
-        for s in range(NQ + 3):
+        nc.scalar.copy(out=bo_b[:, 1:QT, :], in_=bo_b[:, 0, :].unsqueeze(1).to_broadcast([P, QT - 1, DIM]))
+
+        for s in range(NQ - 1):
+            fill = s < LAG
             for half in range(2):
                 for j in range(2 * half, 2 * half + 2):
                     on(st_c, s, j)
+                if fill and half == 0:
+                    st_qh(s + 1)
                 for j in range(2 * half, 2 * half + 2):
-                    on(st_mx2, s - 3, j)
+                    on(st_mx2, s - LAG, j)
             for j in range(QT):
-                on(st_h, s - 3, j)
-            if s - 1 in EDGE:
-                st_nmr(s - 1)
-                st_e(s - 1)
+                on(st_h, s - LAG, j)
+            if s == 0:
+                prep_bf()
+            if fill:
+                for j in range(QT):
+                    st_mx1(s + 1, j)
+                st_xp(s + 1)
             if s == 0:
                 prep_wf_transposes()
             if s == 1:
                 prep_wf_copies()
-            on(st_d, s)
+            st_d(s)
+            if fill:
+                st_rstd(s)
             for t in range(4):
                 on(st_tz, s - 1, t)
-            on(st_gate, s - 3)
-            on(st_xp, s + 1)
-            on(st_qh, s + 1)
+            if not fill:
+                st_gate(s - LAG)
+                st_xp(s + 1)
+                st_qh(s + 1)
             if s == 1:
                 prep_wf_quantise()
-            if s == NQ - 1:
-                st_rstd(s)
             on(st_f, s - 1, 0)
-            if s < NQ - 1:
+            if not fill:
                 st_rstd(s)
             for t in range(1, 4):
                 on(st_f, s - 1, t)
-            for j in range(QT):
-                on(st_mx1, s + 1, j)
+            if not fill:
+                for j in range(QT):
+                    st_mx1(s + 1, j)
             for half in range(2):
                 on(st_th, s + 2, half)
             for half in range(2):
                 on(st_a, s + 2, half)
             on(st_f2, s - 2)
-            on(st_relu, s - 3)
-            if s not in EDGE:
-                on(st_nmr, s)
+            on(st_relu, s - LAG)
+            st_nmr(s)
             on(st_qx, s - 2)
-            if s not in EDGE:
-                on(st_e, s)
+            st_e(s)
             if s % 2 == 0 and (s + 6) // 2 < NCH:
                 load_part(h_tiles, hv, "h", (s + 6) // 2, 0, CH)
                 load_part(x_tiles, xv, "x", (s + 6) // 2, 0, CH)
+
+        q = NQ - 1
+        for half in range(2):
+            for j in range(2 * half, 2 * half + 2):
+                st_c(q, j)
+            for j in range(2 * half, 2 * half + 2):
+                st_mx2(q - 3, j)
+        st_d(q)
+        st_rstd(q)
+        for j in range(QT):
+            st_h(q - 3, j)
+        for t in range(4):
+            st_tz(q - 1, t)
+        for t in range(4):
+            st_f(q - 1, t)
+        st_f2(q - 2)
+        st_nmr(q)
+        st_e(q)
+        st_qx(q - 2)
+        st_f2(q - 1)
+        for j in range(QT):
+            st_mx2(q - 2, j)
+        st_relu(q - 3)
+        for j in range(QT):
+            st_h(q - 2, j)
+        st_qx(q - 1)
+        for t in range(4):
+            st_tz(q, t)
+        for t in range(4):
+            st_f(q, t)
+        st_relu(q - 2)
+        for j in range(QT):
+            st_mx2(q - 1, j)
+        st_h(q - 1, 0)
+        st_h(q - 1, 1)
+        st_f2(q)
+        st_h(q - 1, 2)
+        st_qx(q)
+        st_h(q - 1, 3)
+        st_relu(q - 1)
+        for j in range(QT):
+            st_mx2(q, j)
+        for j in range(QT):
+            st_h(q, j)
+        st_relu(q)

@@ -131,9 +131,18 @@ def tile_l1regressionmoeactionhead_pc_t_kernel(tc, h_attn, x, W_o, b_o, W_ffn, b
 
         S = {}
 
-        def st_xp(q):
+        def st_xp_tile(q):
             xp = work.tile([P, QT, DIM], F32, tag="xp", bufs=2, name="xp")
             S[("xp", q)] = xp
+
+        def st_gate(q):
+            st_xp_tile(q)
+            nc.vector.memset(S[("xp", q)][:, 0, 0:1], 0.0)
+
+        def st_xp(q):
+            if q <= LAG:
+                st_xp_tile(q)
+            xp = S[("xp", q)]
             j0 = (q % 2) * QT
             xq = x_tiles[q // 2]
             if q > LAG:
@@ -229,10 +238,6 @@ def tile_l1regressionmoeactionhead_pc_t_kernel(tc, h_attn, x, W_o, b_o, W_ffn, b
             S[("xc", q)] = (xc, xs)
             nc.vector.quantize_mx(out=xc[:].bitcast(FP8X4), scales=xs[:], in_=S[("xg", q)][:].rearrange("p c t -> p (c t)"))
 
-        def st_gate(q):
-            gate = stats.tile([P, 1], U32, tag="gate", name="gate")
-            nc.gpsimd.tensor_copy(out=gate[:], in_=S[("xc", q)][0][:, 0:1])
-
         def st_mx2(q, j):
             xc, xs = S[("xc", q)]
             p2 = psum.tile([P, DIM], F32, tag="mm", name="p2")
@@ -249,7 +254,7 @@ def tile_l1regressionmoeactionhead_pc_t_kernel(tc, h_attn, x, W_o, b_o, W_ffn, b
         def st_relu(q):
             o = S[("o", q)]
             j0 = (q % 2) * QT
-            if q == NQ - 1:
+            if q >= NQ - 2:
                 for j in range(QT):
                     nc.scalar.activation(out=o[:, j, :], in_=o[:, j, :], func=ACT.Relu)
                     nc.sync.dma_start(out=ov[q // 2][:, j0 + j, :], in_=o[:, j, :])
@@ -308,7 +313,6 @@ def tile_l1regressionmoeactionhead_pc_t_kernel(tc, h_attn, x, W_o, b_o, W_ffn, b
             for t in range(4):
                 on(st_tz, s - 1, t)
             if not fill:
-                st_gate(s - LAG)
                 st_xp(s + 1)
                 st_qh(s + 1)
             if s == 1:
@@ -328,6 +332,8 @@ def tile_l1regressionmoeactionhead_pc_t_kernel(tc, h_attn, x, W_o, b_o, W_ffn, b
             on(st_f2, s - 2)
             on(st_relu, s - LAG)
             st_nmr(s)
+            if s + 2 > LAG:
+                on(st_gate, s + 2)
             on(st_qx, s - 2)
             st_e(s)
             if s % 2 == 0 and (s + 6) // 2 < NCH:

@@ -48,7 +48,11 @@ def tile_l1regressionmoeactionhead_pc_t_kernel(tc, h_attn, x, W_o, b_o, W_ffn, b
             nc.sync.dma_start(out=tiles[c][:, j0:j1, :], in_=view[c][:, j0:j1, :])
 
         wo_sb = const.tile([P, 4, DIM], BF16)
-        nc.sync.dma_start(out=wo_sb[:], in_=W_o.rearrange("(r p) k -> p r k", p=P))
+        wo_view = W_o.rearrange("(r p) k -> p r k", p=P)
+        for half in range(2):
+            nc.sync.dma_start(out=wo_sb[:, 2 * half:2 * half + 2, :], in_=wo_view[:, 2 * half:2 * half + 2, :])
+        ones = const.tile([P, P], BF16)
+        nc.vector.memset(ones[:], 1.0)
         bo_row = const.tile([P, DIM], BF16)
         nc.vector.memset(bo_row[:], 0.0)
         nc.sync.dma_start(out=bo_row[0:1, :], in_=b_o.unsqueeze(0))
@@ -72,8 +76,6 @@ def tile_l1regressionmoeactionhead_pc_t_kernel(tc, h_attn, x, W_o, b_o, W_ffn, b
 
         ident_f = const.tile([P, P], F32)
         make_identity(nc, ident_f[:])
-        ones = const.tile([P, P], BF16)
-        nc.vector.memset(ones[:], 1.0)
         eps_t = const.tile([P, 1], F32)
         nc.vector.memset(eps_t[:], EPS)
         warm = const.tile([P, 1], F32)
@@ -103,11 +105,14 @@ def tile_l1regressionmoeactionhead_pc_t_kernel(tc, h_attn, x, W_o, b_o, W_ffn, b
         wfc = const.tile([P, DIM], U32, align_bytes=64)
         wfs = const.tile([P, DIM], U8, align_bytes=64)
 
-        wt_a = weight_transposes(wo_sb, 0)
-        wt_b = weight_transposes(wo_sb, 1)
-        nc.vector.tensor_copy(out=weight_words(wog, 0), in_=interleaved(wt_a))
-        nc.scalar.copy(out=weight_words(wog, 1), in_=interleaved(wt_b))
-        nc.vector.quantize_mx(out=woc[:].bitcast(FP8X4), scales=wos[:], in_=wog[:])
+        warm_ps = psum.tile([P, DIM], F32, tag="mm", name="warm_ps")
+        for i in range(16):
+            nc.tensor.matmul(warm_ps[:, 0:P], lhsT=ones[:], rhs=ones[:], start=True, stop=True)
+        for half in range(2):
+            wt_o = weight_transposes(wo_sb, half)
+            nc.vector.tensor_copy(out=weight_words(wog, half), in_=interleaved(wt_o))
+            nc.vector.quantize_mx(out=woc[:, half * 2 * P:(half + 1) * 2 * P].bitcast(FP8X4), scales=wos[:, half * 2 * P:(half + 1) * 2 * P],
+                                  in_=wog[:, half * 8 * P:(half + 1) * 8 * P])
 
         wf_ps = []
 
@@ -150,7 +155,7 @@ def tile_l1regressionmoeactionhead_pc_t_kernel(tc, h_attn, x, W_o, b_o, W_ffn, b
                                         in1=bo_b[:].rearrange("p j k -> p (j k)"), op=ALU.add)
                 return
             for j in range(QT):
-                engine = nc.gpsimd if q == 0 and j % 2 == 0 else nc.vector
+                engine = nc.vector if q < 2 and j <= q else nc.gpsimd
                 engine.tensor_tensor(out=xp[:, j, :], in0=xq[:, j0 + j, :], in1=bo_b[:, 0, :], op=ALU.add)
 
         def st_th(q, half):
@@ -168,11 +173,14 @@ def tile_l1regressionmoeactionhead_pc_t_kernel(tc, h_attn, x, W_o, b_o, W_ffn, b
             nc.scalar.copy(out=S[("hg", q)][:].bitcast(F32).rearrange("p (j r u) -> p j r u", j=QT, u=2)[:, 2 * half:2 * half + 2, :, :],
                            in_=S[("ht", q, half)][:].rearrange("p (j u) r -> p j r u", u=2))
 
-        def st_qh(q):
+        def st_qh(q, parts=1):
             hc = work.tile([P, QT * P], U32, tag="hc", bufs=3, align_bytes=64, name="hc")
             hs = work.tile([P, QT * P], U8, tag="hs", bufs=3, align_bytes=64, name="hs")
             S[("hc", q)] = (hc, hs)
-            nc.vector.quantize_mx(out=hc[:].bitcast(FP8X4), scales=hs[:], in_=S[("hg", q)][:])
+            n = QT * P // parts
+            for i in range(parts):
+                cols = slice(i * n, (i + 1) * n)
+                nc.vector.quantize_mx(out=hc[:, cols].bitcast(FP8X4), scales=hs[:, cols], in_=S[("hg", q)][:, 4 * i * n:4 * (i + 1) * n])
 
         def st_mx1(q, j):
             hc, hs = S[("hc", q)]
@@ -269,29 +277,28 @@ def tile_l1regressionmoeactionhead_pc_t_kernel(tc, h_attn, x, W_o, b_o, W_ffn, b
             if 0 <= q < NQ:
                 fn(q, *rest)
 
-        for half in range(2):
-            st_th(0, half)
         bo_ps = psum.tile([P, DIM], F32, tag="mm", name="bo_ps")
         nc.tensor.matmul(bo_ps[:], lhsT=ones[:], rhs=bo_row[:], start=True, stop=True)
+        nc.scalar.copy(out=bo_b[:, 0, :], in_=bo_ps[:])
+        for half in range(2):
+            st_th(0, half)
         for half in range(2):
             st_a(0, half)
-        nc.vector.tensor_copy(out=bo_b[:, 0, :], in_=bo_ps[:])
         for half in range(2):
             st_th(1, half)
-        st_qh(0)
         st_xp(0)
+        st_qh(0, 2)
         for j in range(QT):
             st_mx1(0, j)
         for half in range(2):
             st_a(1, half)
-        nc.scalar.copy(out=bo_b[:, 1:QT, :], in_=bo_b[:, 0, :].unsqueeze(1).to_broadcast([P, QT - 1, DIM]))
 
         for s in range(NQ - 1):
             fill = s < LAG
             for half in range(2):
                 for j in range(2 * half, 2 * half + 2):
                     on(st_c, s, j)
-                if fill and half == 0:
+                if fill and half == min(s, 1):
                     st_qh(s + 1)
                 for j in range(2 * half, 2 * half + 2):
                     on(st_mx2, s - LAG, j)
@@ -303,10 +310,9 @@ def tile_l1regressionmoeactionhead_pc_t_kernel(tc, h_attn, x, W_o, b_o, W_ffn, b
                 for j in range(QT):
                     st_mx1(s + 1, j)
                 st_xp(s + 1)
-            if s == 0:
-                prep_wf_transposes()
             if s == 1:
                 prep_wf_copies()
+                nc.vector.tensor_copy(out=bo_b[:, 1:QT, :], in_=bo_b[:, 0, :].unsqueeze(1).to_broadcast([P, QT - 1, DIM]))
             st_d(s)
             if fill:
                 st_rstd(s)
@@ -327,6 +333,8 @@ def tile_l1regressionmoeactionhead_pc_t_kernel(tc, h_attn, x, W_o, b_o, W_ffn, b
                     st_mx1(s + 1, j)
             for half in range(2):
                 on(st_th, s + 2, half)
+            if s == 0:
+                prep_wf_transposes()
             for half in range(2):
                 on(st_a, s + 2, half)
             on(st_f2, s - 2)

@@ -120,6 +120,8 @@ def tile_l1regressionmoeactionhead_pc_t_kernel(tc, h_attn, x, W_o, b_o, W_ffn, b
             bf_ps = psum.tile([P, DIM], F32, tag="mm", name="bf_ps")
             nc.tensor.matmul(bf_ps[:], lhsT=ones[:], rhs=bf_row[:], start=True, stop=True)
             nc.vector.tensor_copy(out=bf_b[:], in_=bf_ps[:])
+            nc.vector.tensor_copy(out=gb[:, 0:4], in_=g_raw[:])
+            nc.vector.tensor_copy(out=gb[:, 4:8], in_=b_raw[:])
 
         def prep_wf_transposes():
             for half in range(2):
@@ -128,8 +130,6 @@ def tile_l1regressionmoeactionhead_pc_t_kernel(tc, h_attn, x, W_o, b_o, W_ffn, b
         def prep_wf_copies():
             for half in range(2):
                 nc.vector.tensor_copy(out=weight_words(wfg, half), in_=interleaved(wf_ps[half]))
-            nc.vector.tensor_copy(out=gb[:, 0:4], in_=g_raw[:])
-            nc.vector.tensor_copy(out=gb[:, 4:8], in_=b_raw[:])
 
         def prep_wf_quantise():
             nc.vector.quantize_mx(out=wfc[:].bitcast(FP8X4), scales=wfs[:], in_=wfg[:])
@@ -145,18 +145,16 @@ def tile_l1regressionmoeactionhead_pc_t_kernel(tc, h_attn, x, W_o, b_o, W_ffn, b
             nc.vector.memset(S[("xp", q)][:, 0, 0:1], 0.0)
 
         def st_xp(q):
-            if q <= LAG:
-                st_xp_tile(q)
+            share = QT if q > LAG else 2 if q > 0 else 0
             xp = S[("xp", q)]
             j0 = (q % 2) * QT
             xq = x_tiles[q // 2]
-            if q > LAG:
-                nc.gpsimd.tensor_tensor(out=xp[:].rearrange("p j k -> p (j k)"), in0=xq[:, j0:j0 + QT, :].rearrange("p j k -> p (j k)"),
-                                        in1=bo_b[:].rearrange("p j k -> p (j k)"), op=ALU.add)
-                return
-            for j in range(QT):
-                engine = nc.vector if q < 2 and j <= q else nc.gpsimd
-                engine.tensor_tensor(out=xp[:, j, :], in0=xq[:, j0 + j, :], in1=bo_b[:, 0, :], op=ALU.add)
+            if share > 0:
+                nc.gpsimd.tensor_tensor(out=xp[:, 0:share, :].rearrange("p j k -> p (j k)"),
+                                        in0=xq[:, j0:j0 + share, :].rearrange("p j k -> p (j k)"),
+                                        in1=bo_b[:, 0:share, :].rearrange("p j k -> p (j k)"), op=ALU.add)
+            for j in range(share, QT):
+                nc.vector.tensor_tensor(out=xp[:, j, :], in0=xq[:, j0 + j, :], in1=bo_b[:, 0, :], op=ALU.add)
 
         def st_th(q, half):
             ht = psum.tile([P, 4, P], F32, tag="tr", name="ht")
@@ -219,6 +217,10 @@ def tile_l1regressionmoeactionhead_pc_t_kernel(tc, h_attn, x, W_o, b_o, W_ffn, b
         def st_e(q):
             for j in range(QT):
                 y = S[("y", q, j)]
+                if q == NQ - 1:
+                    nc.vector.tensor_scalar(out=y[:], in0=y[:], scalar1=S[("rstd", q)][:, j:j + 1], scalar2=S[("nmr", q)][:, j:j + 1],
+                                            op0=ALU.mult, op1=ALU.add)
+                    continue
                 nc.scalar.activation(out=y[:], in_=y[:], func=ACT.Identity, bias=S[("nmr", q)][:, j:j + 1], scale=S[("rstd", q)][:, j:j + 1])
 
         def st_tz(q, t):
@@ -255,7 +257,7 @@ def tile_l1regressionmoeactionhead_pc_t_kernel(tc, h_attn, x, W_o, b_o, W_ffn, b
 
         def st_h(q, j):
             if j == 0:
-                o = work.tile([P, QT, DIM], F32, tag="o", bufs=3, name="o")
+                o = work.tile([P, QT, DIM], F32, tag="o", bufs=4, name="o")
                 S[("o", q)] = o
             nc.vector.tensor_tensor(out=S[("o", q)][:, j, :], in0=S[("p2", q, j)][:], in1=bf_b[:], op=ALU.add)
 
@@ -267,7 +269,7 @@ def tile_l1regressionmoeactionhead_pc_t_kernel(tc, h_attn, x, W_o, b_o, W_ffn, b
                     nc.scalar.activation(out=o[:, j, :], in_=o[:, j, :], func=ACT.Relu)
                     nc.sync.dma_start(out=ov[q // 2][:, j0 + j, :], in_=o[:, j, :])
                 return
-            if q >= NQ - 3:
+            if q >= NQ - 4:
                 nc.scalar.activation(out=o[:], in_=o[:], func=ACT.Relu)
             else:
                 nc.vector.tensor_scalar(out=o[:], in0=o[:], scalar1=0.0, scalar2=None, op0=ALU.max)
@@ -286,8 +288,11 @@ def tile_l1regressionmoeactionhead_pc_t_kernel(tc, h_attn, x, W_o, b_o, W_ffn, b
             st_a(0, half)
         for half in range(2):
             st_th(1, half)
-        st_xp(0)
         st_qh(0, 2)
+        st_xp_tile(0)
+        st_xp(0)
+        nc.vector.tensor_copy(out=bo_b[:, 1, :], in_=bo_b[:, 0, :])
+        st_gate(1)
         for j in range(QT):
             st_mx1(0, j)
         for half in range(2):
@@ -298,7 +303,7 @@ def tile_l1regressionmoeactionhead_pc_t_kernel(tc, h_attn, x, W_o, b_o, W_ffn, b
             for half in range(2):
                 for j in range(2 * half, 2 * half + 2):
                     on(st_c, s, j)
-                if fill and half == min(s, 1):
+                if fill and half == 1:
                     st_qh(s + 1)
                 for j in range(2 * half, 2 * half + 2):
                     on(st_mx2, s - LAG, j)
@@ -306,13 +311,16 @@ def tile_l1regressionmoeactionhead_pc_t_kernel(tc, h_attn, x, W_o, b_o, W_ffn, b
                 on(st_h, s - LAG, j)
             if s == 0:
                 prep_bf()
+            if s == 0:
+                for half in range(2):
+                    st_th(s + 2, half)
             if fill:
                 for j in range(QT):
                     st_mx1(s + 1, j)
                 st_xp(s + 1)
             if s == 1:
                 prep_wf_copies()
-                nc.vector.tensor_copy(out=bo_b[:, 1:QT, :], in_=bo_b[:, 0, :].unsqueeze(1).to_broadcast([P, QT - 1, DIM]))
+                nc.vector.tensor_copy(out=bo_b[:, 2:QT, :], in_=bo_b[:, 0:2, :])
             st_d(s)
             if fill:
                 st_rstd(s)
@@ -332,7 +340,8 @@ def tile_l1regressionmoeactionhead_pc_t_kernel(tc, h_attn, x, W_o, b_o, W_ffn, b
                 for j in range(QT):
                     st_mx1(s + 1, j)
             for half in range(2):
-                on(st_th, s + 2, half)
+                if s > 0:
+                    on(st_th, s + 2, half)
             if s == 0:
                 prep_wf_transposes()
             for half in range(2):
@@ -340,8 +349,7 @@ def tile_l1regressionmoeactionhead_pc_t_kernel(tc, h_attn, x, W_o, b_o, W_ffn, b
             on(st_f2, s - 2)
             on(st_relu, s - LAG)
             st_nmr(s)
-            if s + 2 > LAG:
-                on(st_gate, s + 2)
+            on(st_gate, s + 2)
             on(st_qx, s - 2)
             st_e(s)
             if s % 2 == 0 and (s + 6) // 2 < NCH:
@@ -367,24 +375,24 @@ def tile_l1regressionmoeactionhead_pc_t_kernel(tc, h_attn, x, W_o, b_o, W_ffn, b
         st_e(q)
         st_qx(q - 2)
         st_f2(q - 1)
+        for t in range(4):
+            st_tz(q, t)
         for j in range(QT):
             st_mx2(q - 2, j)
-        st_relu(q - 3)
         for j in range(QT):
             st_h(q - 2, j)
         st_qx(q - 1)
         for t in range(4):
-            st_tz(q, t)
-        for t in range(4):
             st_f(q, t)
+        st_relu(q - 3)
         st_relu(q - 2)
         for j in range(QT):
             st_mx2(q - 1, j)
+        st_f2(q)
         st_h(q - 1, 0)
         st_h(q - 1, 1)
-        st_f2(q)
-        st_h(q - 1, 2)
         st_qx(q)
+        st_h(q - 1, 2)
         st_h(q - 1, 3)
         st_relu(q - 1)
         for j in range(QT):

from contextlib import ExitStack

import concourse.mybir as mybir
from concourse.masks import make_identity

F32 = mybir.dt.float32
BF16 = mybir.dt.bfloat16
U32 = mybir.dt.uint32
U8 = mybir.dt.uint8
FP8X4 = mybir.dt.float8_e4m3fn_x4
ALU = mybir.AluOpType
ACT = mybir.ActivationFunctionType
ENG = mybir.EngineType

P = 128
DIM = 512
TOKENS = 16 * 512
CH = 8
NCH = TOKENS // (P * CH)
QT = 4
NQ = TOKENS // (P * QT)
LAG = 3
EPS = 1e-5
FLOPS = 2 * 2 * TOKENS * DIM * DIM


def tile_l1regressionmoeactionhead_pc_t_kernel(tc, h_attn, x, W_o, b_o, W_ffn, b_ffn, gamma, beta, out):
    nc = tc.nc
    hv = h_attn.flatten_outer_dims().rearrange("(c p j) k -> c p j k", p=P, j=CH)
    xv = x.flatten_outer_dims().rearrange("(c p j) k -> c p j k", p=P, j=CH)
    ov = out.flatten_outer_dims().rearrange("(c p j) k -> c p j k", p=P, j=CH)

    with ExitStack() as ctx:
        const = ctx.enter_context(tc.tile_pool(name="const", bufs=1))
        loads = ctx.enter_context(tc.tile_pool(name="loads", bufs=3))
        work = ctx.enter_context(tc.tile_pool(name="work", bufs=2))
        stats = ctx.enter_context(tc.tile_pool(name="stats", bufs=4))
        psum = ctx.enter_context(tc.psum_pool(name="psum", bufs=4))
        ctx.enter_context(tc.manual_schedule(engines={ENG.PE, ENG.Activation, ENG.DVE, ENG.Pool}))

        h_tiles = {}
        x_tiles = {}

        def load_part(tiles, view, tag, c, j0, j1):
            if j0 == 0:
                fresh = loads.tile([P, CH, DIM], BF16, tag=tag, name="ld_" + tag)
                tiles[c] = fresh
            nc.sync.dma_start(out=tiles[c][:, j0:j1, :], in_=view[c][:, j0:j1, :])

        wo_sb = const.tile([P, 4, DIM], BF16)
        wo_view = W_o.rearrange("(r p) k -> p r k", p=P)
        for half in range(2):
            nc.sync.dma_start(out=wo_sb[:, 2 * half:2 * half + 2, :], in_=wo_view[:, 2 * half:2 * half + 2, :])
        ones = const.tile([P, P], BF16)
        nc.vector.memset(ones[:], 1.0)
        bo_row = const.tile([P, DIM], BF16)
        nc.vector.memset(bo_row[:], 0.0)
        nc.sync.dma_start(out=bo_row[0:1, :], in_=b_o.unsqueeze(0))
        load_part(h_tiles, hv, "h", 0, 0, 4)
        load_part(x_tiles, xv, "x", 0, 0, 4)
        load_part(h_tiles, hv, "h", 0, 4, 8)
        load_part(x_tiles, xv, "x", 0, 4, 8)
        wf_sb = const.tile([P, 4, DIM], BF16)
        nc.sync.dma_start(out=wf_sb[:], in_=W_ffn.rearrange("(r p) k -> p r k", p=P))
        for c in range(1, 3):
            load_part(h_tiles, hv, "h", c, 0, CH)
            load_part(x_tiles, xv, "x", c, 0, CH)

        bf_row = const.tile([P, DIM], BF16)
        nc.vector.memset(bf_row[:], 0.0)
        nc.scalar.dma_start(out=bf_row[0:1, :], in_=b_ffn.unsqueeze(0))
        g_raw = const.tile([P, 4], BF16)
        nc.scalar.dma_start(out=g_raw[:], in_=gamma.rearrange("(p t) -> p t", t=4))
        b_raw = const.tile([P, 4], BF16)
        nc.scalar.dma_start(out=b_raw[:], in_=beta.rearrange("(p t) -> p t", t=4))

        ident_f = const.tile([P, P], F32)
        make_identity(nc, ident_f[:])
        eps_t = const.tile([P, 1], F32)
        nc.vector.memset(eps_t[:], EPS)
        warm = const.tile([P, 1], F32)
        nc.scalar.activation(out=warm[:], in_=eps_t[:], func=ACT.Abs_reciprocal_sqrt)

        bo_b = const.tile([P, QT, DIM], BF16)
        bf_b = const.tile([P, DIM], BF16)
        gb = const.tile([P, 8], F32)

        def weight_transposes(w_sb, half):
            wt = psum.tile([P, 4, P], F32, tag="tr", name="wt")
            for rr in range(2):
                for u in range(2):
                    nc.tensor.transpose(wt[:, 2 * rr + u, :], w_sb[:, 2 * half + rr, :].bitcast(F32)[:, u::2], ident_f[:])
            return wt

        def weight_words(grouped, half):
            return grouped[:].bitcast(F32).rearrange("p (r c u) -> p r c u", r=4, u=2)[:, 2 * half:2 * half + 2, :, :]

        def interleaved(wt):
            return wt[:].rearrange("p (r u) c -> p r c u", u=2)

        wog = const.tile([P, DIM * 4], BF16, align_bytes=64)
        woc = const.tile([P, DIM], U32, align_bytes=64)
        wos = const.tile([P, DIM], U8, align_bytes=64)
        wfg = const.tile([P, DIM * 4], BF16, align_bytes=64)
        wfc = const.tile([P, DIM], U32, align_bytes=64)
        wfs = const.tile([P, DIM], U8, align_bytes=64)

        warm_ps = psum.tile([P, DIM], F32, tag="mm", name="warm_ps")
        for i in range(16):
            nc.tensor.matmul(warm_ps[:, 0:P], lhsT=ones[:], rhs=ones[:], start=True, stop=True)
        for half in range(2):
            wt_o = weight_transposes(wo_sb, half)
            nc.vector.tensor_copy(out=weight_words(wog, half), in_=interleaved(wt_o))
            nc.vector.quantize_mx(out=woc[:, half * 2 * P:(half + 1) * 2 * P].bitcast(FP8X4), scales=wos[:, half * 2 * P:(half + 1) * 2 * P],
                                  in_=wog[:, half * 8 * P:(half + 1) * 8 * P])

        wf_ps = []

        def prep_bf():
            bf_ps = psum.tile([P, DIM], F32, tag="mm", name="bf_ps")
            nc.tensor.matmul(bf_ps[:], lhsT=ones[:], rhs=bf_row[:], start=True, stop=True)
            nc.vector.tensor_copy(out=bf_b[:], in_=bf_ps[:])
            nc.vector.tensor_copy(out=gb[:, 0:4], in_=g_raw[:])
            nc.vector.tensor_copy(out=gb[:, 4:8], in_=b_raw[:])

        def prep_wf_transposes():
            for half in range(2):
                wf_ps.append(weight_transposes(wf_sb, half))

        def prep_wf_copies():
            for half in range(2):
                nc.vector.tensor_copy(out=weight_words(wfg, half), in_=interleaved(wf_ps[half]))

        def prep_wf_quantise():
            nc.vector.quantize_mx(out=wfc[:].bitcast(FP8X4), scales=wfs[:], in_=wfg[:])

        S = {}

        def st_xp_tile(q):
            xp = work.tile([P, QT, DIM], F32, tag="xp", bufs=2, name="xp")
            S[("xp", q)] = xp

        def st_gate(q):
            st_xp_tile(q)
            nc.vector.memset(S[("xp", q)][:, 0, 0:1], 0.0)

        def st_xp(q):
            share = QT if q > LAG else 2 if q > 0 else 0
            xp = S[("xp", q)]
            j0 = (q % 2) * QT
            xq = x_tiles[q // 2]
            if share > 0:
                nc.gpsimd.tensor_tensor(out=xp[:, 0:share, :].rearrange("p j k -> p (j k)"),
                                        in0=xq[:, j0:j0 + share, :].rearrange("p j k -> p (j k)"),
                                        in1=bo_b[:, 0:share, :].rearrange("p j k -> p (j k)"), op=ALU.add)
            for j in range(share, QT):
                nc.vector.tensor_tensor(out=xp[:, j, :], in0=xq[:, j0 + j, :], in1=bo_b[:, 0, :], op=ALU.add)

        def st_th(q, half):
            ht = psum.tile([P, 4, P], F32, tag="tr", name="ht")
            S[("ht", q, half)] = ht
            for jj in range(2):
                src = h_tiles[q // 2][:, (q % 2) * QT + 2 * half + jj, :].bitcast(F32)
                for u in range(2):
                    nc.tensor.transpose(ht[:, 2 * jj + u, :], src[:, u::2], ident_f[:])

        def st_a(q, half):
            if half == 0:
                hg = work.tile([P, QT * DIM], BF16, tag="hg", bufs=3, align_bytes=64, name="hg")
                S[("hg", q)] = hg
            nc.scalar.copy(out=S[("hg", q)][:].bitcast(F32).rearrange("p (j r u) -> p j r u", j=QT, u=2)[:, 2 * half:2 * half + 2, :, :],
                           in_=S[("ht", q, half)][:].rearrange("p (j u) r -> p j r u", u=2))

        def st_qh(q, parts=1):
            hc = work.tile([P, QT * P], U32, tag="hc", bufs=3, align_bytes=64, name="hc")
            hs = work.tile([P, QT * P], U8, tag="hs", bufs=3, align_bytes=64, name="hs")
            S[("hc", q)] = (hc, hs)
            n = QT * P // parts
            for i in range(parts):
                cols = slice(i * n, (i + 1) * n)
                nc.vector.quantize_mx(out=hc[:, cols].bitcast(FP8X4), scales=hs[:, cols], in_=S[("hg", q)][:, 4 * i * n:4 * (i + 1) * n])

        def st_mx1(q, j):
            hc, hs = S[("hc", q)]
            p1 = psum.tile([P, DIM], F32, tag="mm", name="p1")
            S[("p1", q, j)] = p1
            nc.tensor.matmul_mx(out=p1[:], lhsT=hc[:, j * P:(j + 1) * P].bitcast(FP8X4), lhsT_scale=hs[:, j * P:(j + 1) * P],
                                rhs=woc[:].bitcast(FP8X4), rhs_scale=wos[:], start=True, stop=True)

        def st_c(q, j):
            if j == 0:
                sums = stats.tile([P, QT], F32, tag="sums", name="sums")
                S[("sums", q)] = sums
            y = work.tile([P, DIM], F32, tag="y", bufs=12, name="y")
            S[("y", q, j)] = y
            nc.vector.scalar_tensor_tensor(out=y[:], in0=S[("p1", q, j)][:], scalar=0.0, in1=S[("xp", q)][:, j, :],
                                           op0=ALU.add, op1=ALU.add, accum_out=S[("sums", q)][:, j:j + 1])

        def st_d(q):
            ssq = stats.tile([P, QT], F32, tag="ssq", name="ssq")
            S[("ssq", q)] = ssq
            for j in range(QT):
                junk = work.tile([P, DIM], BF16, tag="junk", name="junk")
                nc.scalar.activation(out=junk[:], in_=S[("y", q, j)][:], func=ACT.Square, bias=S[("sums", q)][:, j:j + 1],
                                     scale=-float(DIM), accum_out=ssq[:, j:j + 1])

        def st_rstd(q):
            rstd = stats.tile([P, QT], F32, tag="rstd", name="rstd")
            S[("rstd", q)] = rstd
            nc.scalar.activation(out=rstd[:], in_=S[("ssq", q)][:], func=ACT.Abs_reciprocal_sqrt, bias=eps_t[:, 0:1], scale=1.0 / DIM ** 3)

        def st_nmr(q):
            nmr = stats.tile([P, QT], F32, tag="nmr", name="nmr")
            S[("nmr", q)] = nmr
            nc.vector.scalar_tensor_tensor(out=nmr[:], in0=S[("sums", q)][:], scalar=-1.0 / DIM, in1=S[("rstd", q)][:], op0=ALU.mult, op1=ALU.mult)

        def st_e(q):
            for j in range(QT):
                y = S[("y", q, j)]
                if q == NQ - 1:
                    nc.vector.tensor_scalar(out=y[:], in0=y[:], scalar1=S[("rstd", q)][:, j:j + 1], scalar2=S[("nmr", q)][:, j:j + 1],
                                            op0=ALU.mult, op1=ALU.add)
                    continue
                nc.scalar.activation(out=y[:], in_=y[:], func=ACT.Identity, bias=S[("nmr", q)][:, j:j + 1], scale=S[("rstd", q)][:, j:j + 1])

        def st_tz(q, t):
            zt = psum.tile([P, QT, P], F32, tag="tr", name="zt")
            S[("zt", q, t)] = zt
            for j in range(QT):
                nc.tensor.transpose(zt[:, j, :], S[("y", q, j)][:, t::4], ident_f[:])

        def st_f(q, t):
            if t == 0:
                planes = work.tile([P, 4, QT * P], BF16, tag="planes", bufs=3, name="planes")
                S[("planes", q)] = planes
            nc.scalar.activation(out=S[("planes", q)][:, t, :], in_=S[("zt", q, t)][:].rearrange("p j r -> p (j r)"),
                                 func=ACT.Identity, bias=gb[:, 4 + t:5 + t], scale=gb[:, t:t + 1])

        def st_f2(q):
            xg = work.tile([P, QT * P, 4], BF16, tag="xg", bufs=2, align_bytes=64, name="xg")
            S[("xg", q)] = xg
            nc.vector.tensor_copy(out=xg[:].rearrange("p (c i) t -> p c t i", i=4),
                                  in_=S[("planes", q)][:].rearrange("p t (c i) -> p c t i", i=4))

        def st_qx(q):
            xc = work.tile([P, QT * P], U32, tag="xc", bufs=3, align_bytes=64, name="xc")
            xs = work.tile([P, QT * P], U8, tag="xs", bufs=3, align_bytes=64, name="xs")
            S[("xc", q)] = (xc, xs)
            nc.vector.quantize_mx(out=xc[:].bitcast(FP8X4), scales=xs[:], in_=S[("xg", q)][:].rearrange("p c t -> p (c t)"))

        def st_mx2(q, j):
            xc, xs = S[("xc", q)]
            p2 = psum.tile([P, DIM], F32, tag="mm", name="p2")
            S[("p2", q, j)] = p2
            nc.tensor.matmul_mx(out=p2[:], lhsT=xc[:, j * P:(j + 1) * P].bitcast(FP8X4), lhsT_scale=xs[:, j * P:(j + 1) * P],
                                rhs=wfc[:].bitcast(FP8X4), rhs_scale=wfs[:], start=True, stop=True)

        def st_h(q, j):
            if j == 0:
                o = work.tile([P, QT, DIM], F32, tag="o", bufs=4, name="o")
                S[("o", q)] = o
            nc.vector.tensor_tensor(out=S[("o", q)][:, j, :], in0=S[("p2", q, j)][:], in1=bf_b[:], op=ALU.add)

        def st_relu(q):
            o = S[("o", q)]
            j0 = (q % 2) * QT
            if q >= NQ - 2:
                for j in range(QT):
                    nc.scalar.activation(out=o[:, j, :], in_=o[:, j, :], func=ACT.Relu)
                    nc.sync.dma_start(out=ov[q // 2][:, j0 + j, :], in_=o[:, j, :])
                return
            if q >= NQ - 4:
                nc.scalar.activation(out=o[:], in_=o[:], func=ACT.Relu)
            else:
                nc.vector.tensor_scalar(out=o[:], in0=o[:], scalar1=0.0, scalar2=None, op0=ALU.max)
            nc.sync.dma_start(out=ov[q // 2][:, j0:j0 + QT, :], in_=o[:])

        def on(fn, q, *rest):
            if 0 <= q < NQ:
                fn(q, *rest)

        bo_ps = psum.tile([P, DIM], F32, tag="mm", name="bo_ps")
        nc.tensor.matmul(bo_ps[:], lhsT=ones[:], rhs=bo_row[:], start=True, stop=True)
        nc.scalar.copy(out=bo_b[:, 0, :], in_=bo_ps[:])
        for half in range(2):
            st_th(0, half)
        for half in range(2):
            st_a(0, half)
        for half in range(2):
            st_th(1, half)
        st_qh(0, 2)
        st_xp_tile(0)
        st_xp(0)
        nc.vector.tensor_copy(out=bo_b[:, 1, :], in_=bo_b[:, 0, :])
        st_gate(1)
        for j in range(QT):
            st_mx1(0, j)
        for half in range(2):
            st_a(1, half)

        for s in range(NQ - 1):
            fill = s < LAG
            for half in range(2):
                for j in range(2 * half, 2 * half + 2):
                    on(st_c, s, j)
                if fill and half == 1:
                    st_qh(s + 1)
                for j in range(2 * half, 2 * half + 2):
                    on(st_mx2, s - LAG, j)
            for j in range(QT):
                on(st_h, s - LAG, j)
            if s == 0:
                prep_bf()
            if s == 0:
                for half in range(2):
                    st_th(s + 2, half)
            if fill:
                for j in range(QT):
                    st_mx1(s + 1, j)
                st_xp(s + 1)
            if s == 1:
                prep_wf_copies()
                nc.vector.tensor_copy(out=bo_b[:, 2:QT, :], in_=bo_b[:, 0:2, :])
            st_d(s)
            if fill:
                st_rstd(s)
            for t in range(4):
                on(st_tz, s - 1, t)
            if not fill:
                st_xp(s + 1)
                st_qh(s + 1)
            if s == 1:
                prep_wf_quantise()
            on(st_f, s - 1, 0)
            if not fill:
                st_rstd(s)
            for t in range(1, 4):
                on(st_f, s - 1, t)
            if not fill:
                for j in range(QT):
                    st_mx1(s + 1, j)
            for half in range(2):
                if s > 0:
                    on(st_th, s + 2, half)
            if s == 0:
                prep_wf_transposes()
            for half in range(2):
                on(st_a, s + 2, half)
            on(st_f2, s - 2)
            on(st_relu, s - LAG)
            st_nmr(s)
            on(st_gate, s + 2)
            on(st_qx, s - 2)
            st_e(s)
            if s % 2 == 0 and (s + 6) // 2 < NCH:
                load_part(h_tiles, hv, "h", (s + 6) // 2, 0, CH)
                load_part(x_tiles, xv, "x", (s + 6) // 2, 0, CH)

        q = NQ - 1
        for half in range(2):
            for j in range(2 * half, 2 * half + 2):
                st_c(q, j)
            for j in range(2 * half, 2 * half + 2):
                st_mx2(q - 3, j)
        st_d(q)
        st_rstd(q)
        for j in range(QT):
            st_h(q - 3, j)
        for t in range(4):
            st_tz(q - 1, t)
        for t in range(4):
            st_f(q - 1, t)
        st_f2(q - 2)
        st_nmr(q)
        st_e(q)
        st_qx(q - 2)
        st_f2(q - 1)
        for t in range(4):
            st_tz(q, t)
        for j in range(QT):
            st_mx2(q - 2, j)
        for j in range(QT):
            st_h(q - 2, j)
        st_qx(q - 1)
        for t in range(4):
            st_f(q, t)
        st_relu(q - 3)
        st_relu(q - 2)
        for j in range(QT):
            st_mx2(q - 1, j)
        st_f2(q)
        st_h(q - 1, 0)
        st_h(q - 1, 1)
        st_qx(q)
        st_h(q - 1, 2)
        st_h(q - 1, 3)
        st_relu(q - 1)
        for j in range(QT):
            st_mx2(q, j)
        for j in range(QT):
            st_h(q, j)
        st_relu(q)
